import numpy as np
import ml_dtypes


def mxq(x, axis, fmt="e4m3"):
    dtype, down = {"e4m3": (ml_dtypes.float8_e4m3fn, 7), "e5m2": (ml_dtypes.float8_e5m2, 14)}[fmt]
    v = np.moveaxis(np.asarray(x, np.float32).astype(ml_dtypes.bfloat16).astype(np.float64), axis, -1)
    blocks = v.reshape(v.shape[:-1] + (-1, 32))
    amax = np.abs(blocks).max(-1, keepdims=True)
    byte = np.maximum(np.where(amax > 0, np.frexp(amax)[1] - 1 + 127, 0) - down, 1)
    scale = np.exp2(byte - 127.0)
    codes = (blocks / scale).astype(np.float32).astype(dtype).astype(np.float64)
    return np.moveaxis((codes * scale).reshape(v.shape), -1, axis)


WIDE = False


def mx_kscale(k):
    if not WIDE:
        return np.ones(k)
    levels = np.array([10, -10, 5, -5, 0])
    a = np.random.permutation(np.resize(levels, k // 512 * 4)).reshape(k // 512, 4)
    idx = np.arange(k)
    return np.exp2(a[idx // 512, idx % 128 // 32])


BF16 = ml_dtypes.bfloat16


def bf(x):
    return np.asarray(x, np.float32).astype(BF16)


def f64(x):
    return np.asarray(x).astype(np.float64)


B, N_OUT, SO, SI, NV, NC, N_PHI, N_DIST, N_SIGMA = 4, 6, 16, 32, 1, 32, 16, 16, 2
DIST_UNIT = 2.0
MIN_SIGMA = 1e-10


def sigmoid(v):
    return 1.0 / (1.0 + np.exp(-v))


def setup_inputs():
    n_in = N_OUT * SO * SI
    a = 2.0 * np.maximum(np.log2(mx_kscale(SO * SI)), 0.0)
    x = bf(np.random.standard_normal((B, n_in, 1, NV, NC)) * 2.0 * np.tile(2.0 ** a, N_OUT)[None, :, None, None, None])
    ux = np.random.uniform(-DIST_UNIT, DIST_UNIT, (1, N_OUT, SO, SI))
    uy = np.random.uniform(-DIST_UNIT, DIST_UNIT, (1, N_OUT, SO, SI))
    phis = bf(np.linspace(-np.pi, np.pi, N_PHI + 1)[:-1] + 0.05 * np.random.standard_normal(N_PHI))
    d = np.arange(1, 2 * N_DIST, 2) / (N_DIST * 2)
    dists_param = bf(-np.log(1.0 / d - 1.0) + 0.1 * np.random.standard_normal(N_DIST))
    s = 0.1 * np.arange(1, N_SIGMA + 1)
    sigma_param = bf(-np.log(1.0 / s - 1.0) + 0.1 * np.random.standard_normal(N_SIGMA))
    dmax = (DIST_UNIT * sigmoid(f64(dists_param))).max()
    smax = (DIST_UNIT * sigmoid(f64(sigma_param))).max()
    A = a.reshape(1, 1, SO, SI)
    R = dmax + smax * np.sqrt(2.0 * np.log(2.0) * A)
    r = np.hypot(ux, uy)
    coords_x = bf(np.where(A > 0, ux / r * R, ux))
    coords_y = bf(np.where(A > 0, uy / r * R, uy))
    return {"x": x, "coords_x": coords_x, "coords_y": coords_y, "phis": phis, "dists_param": dists_param, "sigma_param": sigma_param}


def reference(x, coords_x, coords_y, phis, dists_param, sigma_param):
    x, coords_x, coords_y = f64(x), f64(coords_x), f64(coords_y)
    phis, dists_param, sigma_param = f64(phis), f64(dists_param), f64(sigma_param)
    b = x.shape[0]
    nv, nc = x.shape[-2], x.shape[-1]
    n_out, so, si = coords_x.shape[1], coords_x.shape[2], coords_x.shape[3]
    n_p, n_d, n_s = phis.shape[0], dists_param.shape[0], sigma_param.shape[0]

    dists = DIST_UNIT * sigmoid(dists_param)
    mu_x = np.cos(phis)[:, None] * dists[None, :]
    mu_y = np.sin(phis)[:, None] * dists[None, :]
    sigma = np.maximum(DIST_UNIT * sigmoid(sigma_param), MIN_SIGMA)

    dx = coords_x[0][..., None, None] - mu_x
    dy = coords_y[0][..., None, None] - mu_y
    w = np.exp(-0.5 * (dx * dx + dy * dy)[..., None] / (sigma * sigma))
    w = w / (w.sum(axis=(1, 2), keepdims=True) + 1e-20)

    wq = mxq(w.reshape(n_out, so * si, n_p * n_d * n_s), 1, "e4m3")
    xq = mxq(x.reshape(b, n_out, so * si, nv, nc), 2, "e4m3")
    out = wq.transpose(0, 2, 1)[None, :, None] @ xq.transpose(0, 1, 3, 2, 4)
    return out.reshape(b, n_out, nv, n_p, n_d, n_s, nc)

@@ -1,0 +1,255 @@
+from contextlib import ExitStack
+import math
+
+import concourse.mybir as mybir
+from concourse.masks import make_identity
+
+F32 = mybir.dt.float32
+BF16 = mybir.dt.bfloat16
+U32 = mybir.dt.uint32
+U8 = mybir.dt.uint8
+FP8X4 = mybir.dt.float8_e4m3fn_x4
+ACT = mybir.ActivationFunctionType
+ALU = mybir.AluOpType
+AXIS_X = mybir.AxisListType.X
+
+P = 128
+PACK = 4
+BATCH, NODES, CELLS, CHANNELS = 4, 6, 512, 32
+N_PHI, N_DIST, N_SIGMA = 16, 16, 2
+HALVES = 2
+DIST_PER_HALF = N_DIST // HALVES
+CHUNKS = NODES * HALVES
+COLS = BATCH * CHANNELS
+PER_PARTITION = HALVES * N_SIGMA
+WORDS = CELLS // 2
+DIST_UNIT = 2.0
+MIN_SIGMA = 1e-10
+SUM_EPS = 1e-20
+ROUND_MAGIC = 12582912.0
+NODES_PER_LOAD = 1
+
+FLOPS = 2 * NODES * CELLS * (N_PHI * N_DIST * N_SIGMA) * COLS
+
+
+def tile_polnormal_nolayer_s_kernel(tc, x, coords_x, coords_y, phis, dists_param, sigma_param, out):
+    nc = tc.nc
+    with ExitStack() as ctx:
+        keep = ctx.enter_context(tc.tile_pool(name="keep", bufs=1))
+        work = ctx.enter_context(tc.tile_pool(name="work", bufs=3))
+        psum_flip = ctx.enter_context(tc.psum_pool(name="psum_flip", bufs=3))
+        psum_out = ctx.enter_context(tc.psum_pool(name="psum_out", bufs=2))
+        ctx.enter_context(tc.manual_schedule())
+
+        phis_all = keep.tile([P, N_PHI], BF16)
+        nc.sync.dma_start(out=phis_all[:], in_=phis.partition_broadcast(P))
+        dists_all = keep.tile([P, N_DIST], BF16)
+        nc.sync.dma_start(out=dists_all[:], in_=dists_param.partition_broadcast(P))
+        sigma_all = keep.tile([P, N_SIGMA], BF16)
+        nc.sync.dma_start(out=sigma_all[:], in_=sigma_param.partition_broadcast(P))
+
+        cell_x = keep.tile([P, NODES * CELLS], BF16)
+        cell_y = keep.tile([P, NODES * CELLS], BF16)
+        flat_x = coords_x.rearrange("a o i j -> (a o i j)")
+        flat_y = coords_y.rearrange("a o i j -> (a o i j)")
+        for first in range(0, NODES, NODES_PER_LOAD):
+            cols = slice(first * CELLS, (first + NODES_PER_LOAD) * CELLS)
+            nc.sync.dma_start(out=cell_x[:, cols], in_=flat_x[cols].partition_broadcast(P))
+            nc.sync.dma_start(out=cell_y[:, cols], in_=flat_y[cols].partition_broadcast(P))
+
+        x_raw = keep.tile([P, BATCH * NODES, PACK * CHANNELS], BF16)
+        nc.scalar.dma_start(
+            out=x_raw[:], in_=x.rearrange("b (o q t) a v c -> q (b o) (t a v c)", q=P, t=PACK)
+        )
+
+        ident = keep.tile([P, P], F32)
+        make_identity(nc, ident[:])
+        pick_phi = keep.tile([P, N_PHI], F32)
+        nc.vector.tensor_reduce(
+            out=pick_phi[:], in_=ident[:].rearrange("j (p r) -> j p r", r=DIST_PER_HALF), axis=AXIS_X, op=ALU.add
+        )
+        pick_dist = keep.tile([P, DIST_PER_HALF], F32)
+        nc.vector.tensor_reduce(
+            out=pick_dist[:], in_=ident[:].rearrange("j (p r) -> j r p", r=DIST_PER_HALF), axis=AXIS_X, op=ALU.add
+        )
+
+        phi_terms = keep.tile([P, N_PHI], F32)
+        nc.vector.tensor_mul(out=phi_terms[:], in0=phis_all[:], in1=pick_phi[:])
+        phi = keep.tile([P, 1], F32)
+        nc.vector.tensor_reduce(out=phi[:], in_=phi_terms[:], axis=AXIS_X, op=ALU.add)
+        turn_count = keep.tile([P, 1], F32)
+        nc.vector.tensor_scalar(
+            out=turn_count[:], in0=phi[:], scalar1=1.0 / (2.0 * math.pi), scalar2=ROUND_MAGIC, op0=ALU.mult, op1=ALU.add
+        )
+        whole_turns = keep.tile([P, 1], F32)
+        nc.vector.tensor_scalar(
+            out=whole_turns[:], in0=turn_count[:], scalar1=ROUND_MAGIC, scalar2=2.0 * math.pi,
+            op0=ALU.subtract, op1=ALU.mult,
+        )
+        angles = keep.tile([P, 2], F32)
+        nc.vector.tensor_sub(out=angles[:, 0:1], in0=phi[:], in1=whole_turns[:])
+        angle_size = keep.tile([P, 1], F32)
+        nc.vector.scalar_tensor_tensor(
+            out=angle_size[:], in0=angles[:, 0:1], scalar=-1.0, in1=angles[:, 0:1], op0=ALU.mult, op1=ALU.max
+        )
+        nc.vector.tensor_scalar(
+            out=angles[:, 1:2], in0=angle_size[:], scalar1=-1.0, scalar2=0.5 * math.pi, op0=ALU.mult, op1=ALU.add
+        )
+        sin_cos = keep.tile([P, 2], F32)
+        nc.scalar.activation(out=sin_cos[:], in_=angles[:], func=ACT.Sin)
+
+        dist_terms = keep.tile([P, HALVES, DIST_PER_HALF], F32)
+        nc.vector.tensor_mul(
+            out=dist_terms[:],
+            in0=dists_all[:].rearrange("j (r h) -> j h r", h=HALVES),
+            in1=pick_dist[:].unsqueeze(1).to_broadcast([P, HALVES, DIST_PER_HALF]),
+        )
+        logits = keep.tile([P, HALVES + N_SIGMA], F32)
+        nc.vector.tensor_reduce(out=logits[:, 0:HALVES], in_=dist_terms[:], axis=AXIS_X, op=ALU.add)
+        nc.vector.tensor_copy(out=logits[:, HALVES:], in_=sigma_all[:])
+        lengths = keep.tile([P, HALVES + N_SIGMA], F32)
+        nc.scalar.activation(out=lengths[:], in_=logits[:], func=ACT.Tanh, scale=0.5)
+        nc.vector.tensor_scalar(
+            out=lengths[:], in0=lengths[:], scalar1=0.5 * DIST_UNIT, scalar2=0.5 * DIST_UNIT, op0=ALU.mult, op1=ALU.add
+        )
+
+        neg_mu = keep.tile([P, 2, HALVES], F32)
+        nc.vector.tensor_scalar(
+            out=neg_mu[:, 0, :], in0=lengths[:, 0:HALVES], scalar1=sin_cos[:, 1:2], scalar2=-1.0,
+            op0=ALU.mult, op1=ALU.mult,
+        )
+        nc.vector.tensor_scalar(
+            out=neg_mu[:, 1, :], in0=lengths[:, 0:HALVES], scalar1=sin_cos[:, 0:1], scalar2=-1.0,
+            op0=ALU.mult, op1=ALU.mult,
+        )
+        sigma = keep.tile([P, N_SIGMA], F32)
+        nc.vector.tensor_scalar_max(out=sigma[:], in0=lengths[:, HALVES:], scalar1=MIN_SIGMA)
+        exp_scale = keep.tile([P, N_SIGMA], F32)
+        nc.vector.scalar_tensor_tensor(
+            out=exp_scale[:], in0=sigma[:], scalar=-2.0, in1=sigma[:], op0=ALU.mult, op1=ALU.mult
+        )
+        nc.vector.reciprocal(out=exp_scale[:], in_=exp_scale[:])
+
+        x_grouped = keep.tile([P, NODES, COLS, PACK], BF16, align_bytes=64)
+        x_by_node = x_raw[:].rearrange("q (b o) (t c) -> q o b c t", b=BATCH, t=PACK)
+        x_codes = keep.tile([P, NODES * COLS], U32, align_bytes=64)
+        x_scales = keep.tile([P, NODES * COLS], U8, align_bytes=64)
+
+        def regroup_x(o):
+            nc.vector.tensor_copy(
+                out=x_grouped[:, o].rearrange("q (b c) t -> q b c t", b=BATCH), in_=x_by_node[:, o]
+            )
+
+        def quantise_x(o):
+            node_cols = slice(o * COLS, (o + 1) * COLS)
+            nc.vector.quantize_mx(
+                out=x_codes[:, node_cols].bitcast(FP8X4),
+                scales=x_scales[:, node_cols],
+                in_=x_grouped[:, o].rearrange("q n t -> q (n t)"),
+            )
+
+        squared, dist2, gauss, gauss_sum, flipped, grouped, w_codes, w_scales, products = (
+            {}, {}, {}, {}, {}, {}, {}, {}, {},
+        )
+        out_rows = out.rearrange("b o a p d s c -> b o (a p d s c)")
+
+        def squares(chunk):
+            o, h = divmod(chunk, HALVES)
+            cols = slice(o * CELLS, (o + 1) * CELLS)
+            sq = work.tile([P, 2, CELLS], F32)
+            nc.scalar.activation(out=sq[:, 0, :], in_=cell_x[:, cols], func=ACT.Square, bias=neg_mu[:, 0, h : h + 1])
+            nc.scalar.activation(out=sq[:, 1, :], in_=cell_y[:, cols], func=ACT.Square, bias=neg_mu[:, 1, h : h + 1])
+            squared[chunk] = sq
+
+        def add(chunk):
+            d2 = work.tile([P, CELLS], F32)
+            nc.vector.tensor_add(out=d2[:], in0=squared[chunk][:, 0, :], in1=squared[chunk][:, 1, :])
+            dist2[chunk] = d2
+
+        def exps(chunk):
+            g = work.tile([P, N_SIGMA, CELLS], F32)
+            g_sum = work.tile([P, N_SIGMA], F32)
+            for s in range(N_SIGMA):
+                nc.scalar.activation(
+                    out=g[:, s, :], in_=dist2[chunk][:], func=ACT.Exp, scale=exp_scale[:, s : s + 1],
+                    accum_out=g_sum[:, s : s + 1],
+                )
+            gauss[chunk] = g
+            gauss_sum[chunk] = g_sum
+
+        def normalise_and_flip(chunk):
+            inv_sum = work.tile([P, N_SIGMA], F32)
+            nc.vector.tensor_scalar_add(out=inv_sum[:], in0=gauss_sum[chunk][:], scalar1=SUM_EPS)
+            nc.vector.reciprocal(out=inv_sum[:], in_=inv_sum[:])
+            weights = work.tile([P, N_SIGMA, CELLS], BF16)
+            for s in range(N_SIGMA):
+                nc.vector.tensor_scalar_mul(out=weights[:, s, :], in0=gauss[chunk][:, s, :], scalar1=inv_sum[:, s : s + 1])
+            words = weights[:].bitcast(F32)
+            flip = psum_flip.tile([P, N_SIGMA, 2, P], F32)
+            for s in range(N_SIGMA):
+                for u in range(2):
+                    nc.tensor.transpose(out=flip[:, s, u, :], in_=words[:, s, u:WORDS:2], identity=ident[:])
+            flipped[chunk] = flip
+
+        def regroup(chunk):
+            grp = work.tile([P, N_SIGMA, P, 2], F32, align_bytes=64)
+            nc.vector.tensor_copy(out=grp[:], in_=flipped[chunk][:].rearrange("q s u j -> q s j u"))
+            grouped[chunk] = grp
+
+        def quantise_and_multiply(chunk):
+            o, h = divmod(chunk, HALVES)
+            codes = work.tile([P, N_SIGMA * P], U32, align_bytes=64)
+            scales = work.tile([P, N_SIGMA * P], U8, align_bytes=64)
+            nc.vector.quantize_mx(
+                out=codes[:].bitcast(FP8X4),
+                scales=scales[:],
+                in_=grouped[chunk][:].rearrange("q s j u -> q (s j u)").bitcast(BF16),
+            )
+            if h == 0:
+                product = psum_out.tile([P, PER_PARTITION, COLS], F32)
+                products[o] = product
+            node_cols = slice(o * COLS, (o + 1) * COLS)
+            for s in range(N_SIGMA):
+                comp_cols = slice(s * P, (s + 1) * P)
+                nc.tensor.matmul_mx(
+                    out=products[o][:, h * N_SIGMA + s, :],
+                    lhsT=codes[:, comp_cols].bitcast(FP8X4),
+                    lhsT_scale=scales[:, comp_cols],
+                    rhs=x_codes[:, node_cols].bitcast(FP8X4),
+                    rhs_scale=x_scales[:, node_cols],
+                    start=True,
+                    stop=True,
+                )
+
+        def store(o):
+            result = work.tile([P, BATCH, PER_PARTITION, CHANNELS], F32)
+            nc.vector.tensor_copy(out=result[:], in_=products[o][:].rearrange("j r (b c) -> j b r c", b=BATCH))
+            nc.sync.dma_start(
+                out=out_rows[:, o, :].rearrange("b (j f) -> j b f", j=P),
+                in_=result[:].rearrange("j b r c -> j b (r c)"),
+            )
+
+        squares(0)
+        squares(1)
+        add(0)
+        for chunk in range(CHUNKS):
+            o, h = divmod(chunk, HALVES)
+            exps(chunk)
+            if chunk + 2 < CHUNKS:
+                squares(chunk + 2)
+            if chunk + 1 < CHUNKS:
+                add(chunk + 1)
+            if h == 0:
+                regroup_x(o)
+            if chunk >= 1:
+                regroup(chunk - 1)
+            if chunk >= 3 and h == 1:
+                store(o - 1)
+            normalise_and_flip(chunk)
+            if h == 0:
+                quantise_x(o)
+            if chunk >= 1:
+                quantise_and_multiply(chunk - 1)
+        regroup(CHUNKS - 1)
+        quantise_and_multiply(CHUNKS - 1)
+        store(NODES - 1)

@@ -163,7 +163,7 @@ def tile_polnormal_nolayer_s_kernel(tc, x, coords_x, coords_y, phis, dists_param
 
         def add(chunk):
             d2 = work.tile([P, CELLS], F32)
-            nc.vector.tensor_add(out=d2[:], in0=squared[chunk][:, 0, :], in1=squared[chunk][:, 1, :])
+            nc.gpsimd.tensor_add(out=d2[:], in0=squared[chunk][:, 0, :], in1=squared[chunk][:, 1, :])
             dist2[chunk] = d2
 
         def exps(chunk):

@@ -27,7 +27,6 @@ DIST_UNIT = 2.0
 MIN_SIGMA = 1e-10
 SUM_EPS = 1e-20
 ROUND_MAGIC = 12582912.0
-NODES_PER_LOAD = 1
 
 FLOPS = 2 * NODES * CELLS * (N_PHI * N_DIST * N_SIGMA) * COLS
 
@@ -52,15 +51,13 @@ def tile_polnormal_nolayer_s_kernel(tc, x, coords_x, coords_y, phis, dists_param
         cell_y = keep.tile([P, NODES * CELLS], BF16)
         flat_x = coords_x.rearrange("a o i j -> (a o i j)")
         flat_y = coords_y.rearrange("a o i j -> (a o i j)")
-        for first in range(0, NODES, NODES_PER_LOAD):
-            cols = slice(first * CELLS, (first + NODES_PER_LOAD) * CELLS)
+        x_raw = keep.tile([P, NODES, BATCH, PACK * CHANNELS], BF16)
+        x_cells = x.rearrange("b (o q t) a v c -> o q b (t a v c)", q=P, t=PACK)
+        for o in range(NODES):
+            cols = slice(o * CELLS, (o + 1) * CELLS)
             nc.sync.dma_start(out=cell_x[:, cols], in_=flat_x[cols].partition_broadcast(P))
             nc.sync.dma_start(out=cell_y[:, cols], in_=flat_y[cols].partition_broadcast(P))
-
-        x_raw = keep.tile([P, BATCH * NODES, PACK * CHANNELS], BF16)
-        nc.scalar.dma_start(
-            out=x_raw[:], in_=x.rearrange("b (o q t) a v c -> q (b o) (t a v c)", q=P, t=PACK)
-        )
+            nc.sync.dma_start(out=x_raw[:, o], in_=x_cells[o])
 
         ident = keep.tile([P, P], F32)
         make_identity(nc, ident[:])
@@ -131,7 +128,7 @@ def tile_polnormal_nolayer_s_kernel(tc, x, coords_x, coords_y, phis, dists_param
         nc.vector.reciprocal(out=exp_scale[:], in_=exp_scale[:])
 
         x_grouped = keep.tile([P, NODES, COLS, PACK], BF16, align_bytes=64)
-        x_by_node = x_raw[:].rearrange("q (b o) (t c) -> q o b c t", b=BATCH, t=PACK)
+        x_by_node = x_raw[:].rearrange("q o b (t c) -> q o b c t", t=PACK)
         x_codes = keep.tile([P, NODES * COLS], U32, align_bytes=64)
         x_scales = keep.tile([P, NODES * COLS], U8, align_bytes=64)
 
@@ -163,7 +160,7 @@ def tile_polnormal_nolayer_s_kernel(tc, x, coords_x, coords_y, phis, dists_param
 
         def add(chunk):
             d2 = work.tile([P, CELLS], F32)
-            nc.gpsimd.tensor_add(out=d2[:], in0=squared[chunk][:, 0, :], in1=squared[chunk][:, 1, :])
+            nc.vector.tensor_add(out=d2[:], in0=squared[chunk][:, 0, :], in1=squared[chunk][:, 1, :])
             dist2[chunk] = d2
 
         def exps(chunk):
@@ -232,24 +229,26 @@ def tile_polnormal_nolayer_s_kernel(tc, x, coords_x, coords_y, phis, dists_param
         squares(0)
         squares(1)
         add(0)
+        add(1)
+        regroup_x(0)
+        quantise_x(0)
         for chunk in range(CHUNKS):
             o, h = divmod(chunk, HALVES)
             exps(chunk)
             if chunk + 2 < CHUNKS:
                 squares(chunk + 2)
-            if chunk + 1 < CHUNKS:
-                add(chunk + 1)
-            if h == 0:
-                regroup_x(o)
-            if chunk >= 1:
-                regroup(chunk - 1)
-            if chunk >= 3 and h == 1:
-                store(o - 1)
             normalise_and_flip(chunk)
-            if h == 0:
-                quantise_x(o)
             if chunk >= 1:
                 quantise_and_multiply(chunk - 1)
-        regroup(CHUNKS - 1)
+            if o + 1 < NODES:
+                if h == 0:
+                    regroup_x(o + 1)
+                else:
+                    quantise_x(o + 1)
+            if h == 1 and o >= 1:
+                store(o - 1)
+            if chunk + 2 < CHUNKS:
+                add(chunk + 2)
+            regroup(chunk)
         quantise_and_multiply(CHUNKS - 1)
         store(NODES - 1)

@@ -26,6 +26,7 @@ WORDS = CELLS // 2
 DIST_UNIT = 2.0
 MIN_SIGMA = 1e-10
 SUM_EPS = 1e-20
+X_FIRST = 4
 ROUND_MAGIC = 12582912.0
 
 FLOPS = 2 * NODES * CELLS * (N_PHI * N_DIST * N_SIGMA) * COLS
@@ -53,11 +54,17 @@ def tile_polnormal_nolayer_s_kernel(tc, x, coords_x, coords_y, phis, dists_param
         flat_y = coords_y.rearrange("a o i j -> (a o i j)")
         x_raw = keep.tile([P, NODES, BATCH, PACK * CHANNELS], BF16)
         x_cells = x.rearrange("b (o q t) a v c -> o q b (t a v c)", q=P, t=PACK)
-        for o in range(NODES):
+
+        def load_positions(o):
             cols = slice(o * CELLS, (o + 1) * CELLS)
             nc.sync.dma_start(out=cell_x[:, cols], in_=flat_x[cols].partition_broadcast(P))
             nc.sync.dma_start(out=cell_y[:, cols], in_=flat_y[cols].partition_broadcast(P))
+
+        load_positions(0)
+        for o in range(NODES):
             nc.sync.dma_start(out=x_raw[:, o], in_=x_cells[o])
+        for o in range(1, NODES):
+            load_positions(o)
 
         ident = keep.tile([P, P], F32)
         make_identity(nc, ident[:])
@@ -127,22 +134,23 @@ def tile_polnormal_nolayer_s_kernel(tc, x, coords_x, coords_y, phis, dists_param
         )
         nc.vector.reciprocal(out=exp_scale[:], in_=exp_scale[:])
 
-        x_grouped = keep.tile([P, NODES, COLS, PACK], BF16, align_bytes=64)
-        x_by_node = x_raw[:].rearrange("q o b (t c) -> q o b c t", t=PACK)
+        x_grouped = keep.tile([P, NODES * BATCH, CHANNELS, PACK], BF16, align_bytes=64)
         x_codes = keep.tile([P, NODES * COLS], U32, align_bytes=64)
         x_scales = keep.tile([P, NODES * COLS], U8, align_bytes=64)
 
-        def regroup_x(o):
+        def regroup_x(first, count):
+            rows = slice(first * BATCH, (first + count) * BATCH)
             nc.vector.tensor_copy(
-                out=x_grouped[:, o].rearrange("q (b c) t -> q b c t", b=BATCH), in_=x_by_node[:, o]
+                out=x_grouped[:, rows], in_=x_raw[:].rearrange("q o b (t c) -> q (o b) c t", t=PACK)[:, rows]
             )
 
-        def quantise_x(o):
-            node_cols = slice(o * COLS, (o + 1) * COLS)
+        def quantise_x(first, count):
+            rows = slice(first * BATCH, (first + count) * BATCH)
+            cols = slice(first * COLS, (first + count) * COLS)
             nc.vector.quantize_mx(
-                out=x_codes[:, node_cols].bitcast(FP8X4),
-                scales=x_scales[:, node_cols],
-                in_=x_grouped[:, o].rearrange("q n t -> q (n t)"),
+                out=x_codes[:, cols].bitcast(FP8X4),
+                scales=x_scales[:, cols],
+                in_=x_grouped[:, rows].rearrange("q n c t -> q (n c t)"),
             )
 
         squared, dist2, gauss, gauss_sum, flipped, grouped, w_codes, w_scales, products = (
@@ -220,7 +228,11 @@ def tile_polnormal_nolayer_s_kernel(tc, x, coords_x, coords_y, phis, dists_param
 
         def store(o):
             result = work.tile([P, BATCH, PER_PARTITION, CHANNELS], F32)
-            nc.vector.tensor_copy(out=result[:], in_=products[o][:].rearrange("j r (b c) -> j b r c", b=BATCH))
+            by_batch = products[o][:].rearrange("j r (b c) -> j b r c", b=BATCH)
+            if o % 2 == 0:
+                nc.scalar.copy(out=result[:], in_=by_batch)
+            else:
+                nc.vector.tensor_copy(out=result[:], in_=by_batch)
             nc.sync.dma_start(
                 out=out_rows[:, o, :].rearrange("b (j f) -> j b f", j=P),
                 in_=result[:].rearrange("j b r c -> j b (r c)"),
@@ -228,10 +240,12 @@ def tile_polnormal_nolayer_s_kernel(tc, x, coords_x, coords_y, phis, dists_param
 
         squares(0)
         squares(1)
+        regroup_x(0, X_FIRST)
         add(0)
+        regroup_x(X_FIRST, NODES - X_FIRST)
         add(1)
-        regroup_x(0)
-        quantise_x(0)
+        quantise_x(0, X_FIRST)
+        quantise_x(X_FIRST, NODES - X_FIRST)
         for chunk in range(CHUNKS):
             o, h = divmod(chunk, HALVES)
             exps(chunk)
@@ -239,16 +253,13 @@ def tile_polnormal_nolayer_s_kernel(tc, x, coords_x, coords_y, phis, dists_param
                 squares(chunk + 2)
             normalise_and_flip(chunk)
             if chunk >= 1:
-                quantise_and_multiply(chunk - 1)
-            if o + 1 < NODES:
-                if h == 0:
-                    regroup_x(o + 1)
-                else:
-                    quantise_x(o + 1)
-            if h == 1 and o >= 1:
-                store(o - 1)
+                regroup(chunk - 1)
             if chunk + 2 < CHUNKS:
                 add(chunk + 2)
-            regroup(chunk)
+            if chunk >= 1:
+                quantise_and_multiply(chunk - 1)
+            if h == 1 and o >= 1:
+                store(o - 1)
+        regroup(CHUNKS - 1)
         quantise_and_multiply(CHUNKS - 1)
         store(NODES - 1)

@@ -8,6 +8,7 @@ F32 = mybir.dt.float32
 BF16 = mybir.dt.bfloat16
 U32 = mybir.dt.uint32
 U8 = mybir.dt.uint8
+I32 = mybir.dt.int32
 FP8X4 = mybir.dt.float8_e4m3fn_x4
 ACT = mybir.ActivationFunctionType
 ALU = mybir.AluOpType
@@ -20,6 +21,9 @@ N_PHI, N_DIST, N_SIGMA = 16, 16, 2
 HALVES = 2
 DIST_PER_HALF = N_DIST // HALVES
 CHUNKS = NODES * HALVES
+BLOCKS_PER_NODE = CELLS // P
+BLOCKS = NODES * BLOCKS_PER_NODE
+Y_ROW = 32
 COLS = BATCH * CHANNELS
 PER_PARTITION = HALVES * N_SIGMA
 WORDS = CELLS // 2
@@ -39,6 +43,7 @@ def tile_polnormal_nolayer_s_kernel(tc, x, coords_x, coords_y, phis, dists_param
         work = ctx.enter_context(tc.tile_pool(name="work", bufs=3))
         psum_flip = ctx.enter_context(tc.psum_pool(name="psum_flip", bufs=3))
         psum_out = ctx.enter_context(tc.psum_pool(name="psum_out", bufs=2))
+        psum_table = ctx.enter_context(tc.psum_pool(name="psum_table", bufs=2))
         ctx.enter_context(tc.manual_schedule())
 
         phis_all = keep.tile([P, N_PHI], BF16)
@@ -48,26 +53,24 @@ def tile_polnormal_nolayer_s_kernel(tc, x, coords_x, coords_y, phis, dists_param
         sigma_all = keep.tile([P, N_SIGMA], BF16)
         nc.sync.dma_start(out=sigma_all[:], in_=sigma_param.partition_broadcast(P))
 
-        cell_x = keep.tile([P, NODES * CELLS], BF16)
-        cell_y = keep.tile([P, NODES * CELLS], BF16)
-        flat_x = coords_x.rearrange("a o i j -> (a o i j)")
-        flat_y = coords_y.rearrange("a o i j -> (a o i j)")
+        coord_rows = keep.tile([P, P], BF16)
+        nc.vector.memset(coord_rows[:].bitcast(I32), 0)
+        nc.sync.dma_start(
+            out=coord_rows[0:BLOCKS, :], in_=coords_x.rearrange("a o (kb i) j -> (a o kb) (i j)", kb=BLOCKS_PER_NODE)
+        )
+        nc.sync.dma_start(
+            out=coord_rows[Y_ROW : Y_ROW + BLOCKS, :],
+            in_=coords_y.rearrange("a o (kb i) j -> (a o kb) (i j)", kb=BLOCKS_PER_NODE),
+        )
         x_raw = keep.tile([P, NODES, BATCH, PACK * CHANNELS], BF16)
         x_cells = x.rearrange("b (o q t) a v c -> o q b (t a v c)", q=P, t=PACK)
-
-        def load_positions(o):
-            cols = slice(o * CELLS, (o + 1) * CELLS)
-            nc.sync.dma_start(out=cell_x[:, cols], in_=flat_x[cols].partition_broadcast(P))
-            nc.sync.dma_start(out=cell_y[:, cols], in_=flat_y[cols].partition_broadcast(P))
-
-        load_positions(0)
         for o in range(NODES):
             nc.sync.dma_start(out=x_raw[:, o], in_=x_cells[o])
-        for o in range(1, NODES):
-            load_positions(o)
 
         ident = keep.tile([P, P], F32)
         make_identity(nc, ident[:])
+        ident_bf = keep.tile([P, P], BF16)
+        nc.vector.tensor_copy(out=ident_bf[:], in_=ident[:])
         pick_phi = keep.tile([P, N_PHI], F32)
         nc.vector.tensor_reduce(
             out=pick_phi[:], in_=ident[:].rearrange("j (p r) -> j p r", r=DIST_PER_HALF), axis=AXIS_X, op=ALU.add
@@ -101,6 +104,11 @@ def tile_polnormal_nolayer_s_kernel(tc, x, coords_x, coords_y, phis, dists_param
         )
         sin_cos = keep.tile([P, 2], F32)
         nc.scalar.activation(out=sin_cos[:], in_=angles[:], func=ACT.Sin)
+
+        turned = psum_table.tile([P, P], BF16, tag="table")
+        nc.tensor.transpose(out=turned[:], in_=coord_rows[:], identity=ident_bf[:])
+        cell_pos = keep.tile([P, P], BF16)
+        nc.vector.tensor_copy(out=cell_pos[:], in_=turned[:])
 
         dist_terms = keep.tile([P, HALVES, DIST_PER_HALF], F32)
         nc.vector.tensor_mul(
@@ -153,17 +161,28 @@ def tile_polnormal_nolayer_s_kernel(tc, x, coords_x, coords_y, phis, dists_param
                 in_=x_grouped[:, rows].rearrange("q n c t -> q (n c t)"),
             )
 
-        squared, dist2, gauss, gauss_sum, flipped, grouped, w_codes, w_scales, products = (
-            {}, {}, {}, {}, {}, {}, {}, {}, {},
-        )
+        tables, squared, dist2, gauss, gauss_sum, flipped, grouped, products = ({}, {}, {}, {}, {}, {}, {}, {})
         out_rows = out.rearrange("b o a p d s c -> b o (a p d s c)")
+
+        def spread(o):
+            table = psum_table.tile([P, 2, CELLS], BF16, tag="table")
+            for axis in range(2):
+                for kb in range(BLOCKS_PER_NODE):
+                    row = axis * Y_ROW + o * BLOCKS_PER_NODE + kb
+                    nc.tensor.transpose(
+                        out=table[:, axis, kb * P : (kb + 1) * P],
+                        in_=cell_pos[:, row : row + 1].to_broadcast([P, P]),
+                        identity=ident_bf[:],
+                    )
+            tables[o] = table
 
         def squares(chunk):
             o, h = divmod(chunk, HALVES)
-            cols = slice(o * CELLS, (o + 1) * CELLS)
             sq = work.tile([P, 2, CELLS], F32)
-            nc.scalar.activation(out=sq[:, 0, :], in_=cell_x[:, cols], func=ACT.Square, bias=neg_mu[:, 0, h : h + 1])
-            nc.scalar.activation(out=sq[:, 1, :], in_=cell_y[:, cols], func=ACT.Square, bias=neg_mu[:, 1, h : h + 1])
+            for axis in range(2):
+                nc.scalar.activation(
+                    out=sq[:, axis, :], in_=tables[o][:, axis, :], func=ACT.Square, bias=neg_mu[:, axis, h : h + 1]
+                )
             squared[chunk] = sq
 
         def add(chunk):
@@ -238,6 +257,8 @@ def tile_polnormal_nolayer_s_kernel(tc, x, coords_x, coords_y, phis, dists_param
                 in_=result[:].rearrange("j b r c -> j b (r c)"),
             )
 
+        spread(0)
+        spread(1)
         squares(0)
         squares(1)
         regroup_x(0, X_FIRST)
@@ -248,6 +269,8 @@ def tile_polnormal_nolayer_s_kernel(tc, x, coords_x, coords_y, phis, dists_param
         quantise_x(X_FIRST, NODES - X_FIRST)
         for chunk in range(CHUNKS):
             o, h = divmod(chunk, HALVES)
+            if h == 1 and o + 2 < NODES:
+                spread(o + 2)
             exps(chunk)
             if chunk + 2 < CHUNKS:
                 squares(chunk + 2)

@@ -80,30 +80,28 @@ def tile_polnormal_nolayer_s_kernel(tc, x, coords_x, coords_y, phis, dists_param
             out=pick_dist[:], in_=ident[:].rearrange("j (p r) -> j r p", r=DIST_PER_HALF), axis=AXIS_X, op=ALU.add
         )
 
+        turn_offset = keep.tile([P, 2], F32)
+        nc.vector.memset(turn_offset[:, 0:1], 0.25)
+        nc.vector.memset(turn_offset[:, 1:2], 0.0)
+        to_neg_dir = keep.tile([P, 2], F32)
+        nc.vector.memset(to_neg_dir[:, 0:1], 0.5 * DIST_UNIT)
+        nc.vector.memset(to_neg_dir[:, 1:2], -0.5 * DIST_UNIT)
+
         phi_terms = keep.tile([P, N_PHI], F32)
         nc.vector.tensor_mul(out=phi_terms[:], in0=phis_all[:], in1=pick_phi[:])
         phi = keep.tile([P, 1], F32)
         nc.vector.tensor_reduce(out=phi[:], in_=phi_terms[:], axis=AXIS_X, op=ALU.add)
-        turn_count = keep.tile([P, 1], F32)
-        nc.vector.tensor_scalar(
-            out=turn_count[:], in0=phi[:], scalar1=1.0 / (2.0 * math.pi), scalar2=ROUND_MAGIC, op0=ALU.mult, op1=ALU.add
-        )
-        whole_turns = keep.tile([P, 1], F32)
-        nc.vector.tensor_scalar(
-            out=whole_turns[:], in0=turn_count[:], scalar1=ROUND_MAGIC, scalar2=2.0 * math.pi,
-            op0=ALU.subtract, op1=ALU.mult,
-        )
-        angles = keep.tile([P, 2], F32)
-        nc.vector.tensor_sub(out=angles[:, 0:1], in0=phi[:], in1=whole_turns[:])
-        angle_size = keep.tile([P, 1], F32)
+        turns = keep.tile([P, 2], F32)
         nc.vector.scalar_tensor_tensor(
-            out=angle_size[:], in0=angles[:, 0:1], scalar=-1.0, in1=angles[:, 0:1], op0=ALU.mult, op1=ALU.max
+            out=turns[:], in0=phi[:, 0:1].to_broadcast([P, 2]), scalar=1.0 / (2.0 * math.pi), in1=turn_offset[:],
+            op0=ALU.mult, op1=ALU.subtract,
         )
         nc.vector.tensor_scalar(
-            out=angles[:, 1:2], in0=angle_size[:], scalar1=-1.0, scalar2=0.5 * math.pi, op0=ALU.mult, op1=ALU.add
+            out=turns[:], in0=turns[:], scalar1=ROUND_MAGIC, scalar2=ROUND_MAGIC, op0=ALU.add, op1=ALU.subtract
         )
-        sin_cos = keep.tile([P, 2], F32)
-        nc.scalar.activation(out=sin_cos[:], in_=angles[:], func=ACT.Sin)
+        nc.vector.tensor_add(out=turns[:], in0=turns[:], in1=turn_offset[:])
+        neg_dir = keep.tile([P, 2], F32)
+        nc.scalar.activation(out=neg_dir[:], in_=turns[:], func=ACT.Sin, scale=-2.0 * math.pi, bias=phi[:, 0:1])
 
         turned = psum_table.tile([P, P], BF16, tag="table")
         nc.tensor.transpose(out=turned[:], in_=coord_rows[:], identity=ident_bf[:])
@@ -119,23 +117,21 @@ def tile_polnormal_nolayer_s_kernel(tc, x, coords_x, coords_y, phis, dists_param
         logits = keep.tile([P, HALVES + N_SIGMA], F32)
         nc.vector.tensor_reduce(out=logits[:, 0:HALVES], in_=dist_terms[:], axis=AXIS_X, op=ALU.add)
         nc.vector.tensor_copy(out=logits[:, HALVES:], in_=sigma_all[:])
-        lengths = keep.tile([P, HALVES + N_SIGMA], F32)
-        nc.scalar.activation(out=lengths[:], in_=logits[:], func=ACT.Tanh, scale=0.5)
-        nc.vector.tensor_scalar(
-            out=lengths[:], in0=lengths[:], scalar1=0.5 * DIST_UNIT, scalar2=0.5 * DIST_UNIT, op0=ALU.mult, op1=ALU.add
-        )
+        tanh_half = keep.tile([P, HALVES + N_SIGMA], F32)
+        nc.scalar.activation(out=tanh_half[:], in_=logits[:], func=ACT.Tanh, scale=0.5)
+        nc.vector.tensor_mul(out=neg_dir[:], in0=neg_dir[:], in1=to_neg_dir[:])
 
         neg_mu = keep.tile([P, 2, HALVES], F32)
-        nc.vector.tensor_scalar(
-            out=neg_mu[:, 0, :], in0=lengths[:, 0:HALVES], scalar1=sin_cos[:, 1:2], scalar2=-1.0,
-            op0=ALU.mult, op1=ALU.mult,
-        )
-        nc.vector.tensor_scalar(
-            out=neg_mu[:, 1, :], in0=lengths[:, 0:HALVES], scalar1=sin_cos[:, 0:1], scalar2=-1.0,
-            op0=ALU.mult, op1=ALU.mult,
-        )
+        for axis in range(2):
+            nc.vector.tensor_scalar(
+                out=neg_mu[:, axis, :], in0=tanh_half[:, 0:HALVES], scalar1=1.0, scalar2=neg_dir[:, axis : axis + 1],
+                op0=ALU.add, op1=ALU.mult,
+            )
         sigma = keep.tile([P, N_SIGMA], F32)
-        nc.vector.tensor_scalar_max(out=sigma[:], in0=lengths[:, HALVES:], scalar1=MIN_SIGMA)
+        nc.vector.tensor_scalar(
+            out=sigma[:], in0=tanh_half[:, HALVES:], scalar1=1.0, scalar2=0.5 * DIST_UNIT, op0=ALU.add, op1=ALU.mult
+        )
+        nc.vector.tensor_scalar_max(out=sigma[:], in0=sigma[:], scalar1=MIN_SIGMA)
         exp_scale = keep.tile([P, N_SIGMA], F32)
         nc.vector.scalar_tensor_tensor(
             out=exp_scale[:], in0=sigma[:], scalar=-2.0, in1=sigma[:], op0=ALU.mult, op1=ALU.mult
@@ -161,7 +157,9 @@ def tile_polnormal_nolayer_s_kernel(tc, x, coords_x, coords_y, phis, dists_param
                 in_=x_grouped[:, rows].rearrange("q n c t -> q (n c t)"),
             )
 
-        tables, squared, dist2, gauss, gauss_sum, flipped, grouped, products = ({}, {}, {}, {}, {}, {}, {}, {})
+        tables, squared, dist2, gauss, gauss_sum, padded_sum, inv_sum, flipped, grouped, products = (
+            {}, {}, {}, {}, {}, {}, {}, {}, {}, {},
+        )
         out_rows = out.rearrange("b o a p d s c -> b o (a p d s c)")
 
         def spread(o):
@@ -201,13 +199,22 @@ def tile_polnormal_nolayer_s_kernel(tc, x, coords_x, coords_y, phis, dists_param
             gauss[chunk] = g
             gauss_sum[chunk] = g_sum
 
+        def pad_sums(chunk):
+            padded = work.tile([P, N_SIGMA], F32)
+            nc.vector.tensor_scalar_add(out=padded[:], in0=gauss_sum[chunk][:], scalar1=SUM_EPS)
+            padded_sum[chunk] = padded
+
+        def invert_sums(chunk):
+            inv = work.tile([P, N_SIGMA], F32)
+            nc.vector.reciprocal(out=inv[:], in_=padded_sum[chunk][:])
+            inv_sum[chunk] = inv
+
         def normalise_and_flip(chunk):
-            inv_sum = work.tile([P, N_SIGMA], F32)
-            nc.vector.tensor_scalar_add(out=inv_sum[:], in0=gauss_sum[chunk][:], scalar1=SUM_EPS)
-            nc.vector.reciprocal(out=inv_sum[:], in_=inv_sum[:])
             weights = work.tile([P, N_SIGMA, CELLS], BF16)
             for s in range(N_SIGMA):
-                nc.vector.tensor_scalar_mul(out=weights[:, s, :], in0=gauss[chunk][:, s, :], scalar1=inv_sum[:, s : s + 1])
+                nc.vector.tensor_scalar_mul(
+                    out=weights[:, s, :], in0=gauss[chunk][:, s, :], scalar1=inv_sum[chunk][:, s : s + 1]
+                )
             words = weights[:].bitcast(F32)
             flip = psum_flip.tile([P, N_SIGMA, 2, P], F32)
             for s in range(N_SIGMA):
@@ -264,7 +271,6 @@ def tile_polnormal_nolayer_s_kernel(tc, x, coords_x, coords_y, phis, dists_param
         regroup_x(0, X_FIRST)
         add(0)
         regroup_x(X_FIRST, NODES - X_FIRST)
-        add(1)
         quantise_x(0, X_FIRST)
         quantise_x(X_FIRST, NODES - X_FIRST)
         for chunk in range(CHUNKS):
@@ -274,11 +280,13 @@ def tile_polnormal_nolayer_s_kernel(tc, x, coords_x, coords_y, phis, dists_param
             exps(chunk)
             if chunk + 2 < CHUNKS:
                 squares(chunk + 2)
-            normalise_and_flip(chunk)
+            pad_sums(chunk)
+            if chunk + 1 < CHUNKS:
+                add(chunk + 1)
+            invert_sums(chunk)
             if chunk >= 1:
                 regroup(chunk - 1)
-            if chunk + 2 < CHUNKS:
-                add(chunk + 2)
+            normalise_and_flip(chunk)
             if chunk >= 1:
                 quantise_and_multiply(chunk - 1)
             if h == 1 and o >= 1:

@@ -30,6 +30,7 @@ WORDS = CELLS // 2
 DIST_UNIT = 2.0
 MIN_SIGMA = 1e-10
 SUM_EPS = 1e-20
+SCALAR_STORES = 2
 X_FIRST = 4
 ROUND_MAGIC = 12582912.0
 
@@ -80,26 +81,35 @@ def tile_polnormal_nolayer_s_kernel(tc, x, coords_x, coords_y, phis, dists_param
             out=pick_dist[:], in_=ident[:].rearrange("j (p r) -> j r p", r=DIST_PER_HALF), axis=AXIS_X, op=ALU.add
         )
 
+        pick_turns = keep.tile([P, N_PHI], F32)
+        nc.vector.tensor_scalar_mul(out=pick_turns[:], in0=pick_phi[:], scalar1=1.0 / (2.0 * math.pi))
         turn_offset = keep.tile([P, 2], F32)
         nc.vector.memset(turn_offset[:, 0:1], 0.25)
         nc.vector.memset(turn_offset[:, 1:2], 0.0)
+        neg_turn_offset = keep.tile([P, 2], F32)
+        nc.vector.memset(neg_turn_offset[:, 0:1], -0.25)
+        nc.vector.memset(neg_turn_offset[:, 1:2], 0.0)
         to_neg_dir = keep.tile([P, 2], F32)
         nc.vector.memset(to_neg_dir[:, 0:1], 0.5 * DIST_UNIT)
         nc.vector.memset(to_neg_dir[:, 1:2], -0.5 * DIST_UNIT)
 
+        turn_terms = keep.tile([P, N_PHI], F32)
+        nc.vector.tensor_mul(out=turn_terms[:], in0=phis_all[:], in1=pick_turns[:])
         phi_terms = keep.tile([P, N_PHI], F32)
         nc.vector.tensor_mul(out=phi_terms[:], in0=phis_all[:], in1=pick_phi[:])
+        phi_turns = keep.tile([P, 1], F32)
+        nc.vector.tensor_reduce(out=phi_turns[:], in_=turn_terms[:], axis=AXIS_X, op=ALU.add)
         phi = keep.tile([P, 1], F32)
         nc.vector.tensor_reduce(out=phi[:], in_=phi_terms[:], axis=AXIS_X, op=ALU.add)
+        shifted = keep.tile([P, 2], F32)
+        nc.vector.tensor_scalar(
+            out=shifted[:], in0=neg_turn_offset[:], scalar1=phi_turns[:, 0:1], scalar2=ROUND_MAGIC,
+            op0=ALU.add, op1=ALU.add,
+        )
         turns = keep.tile([P, 2], F32)
         nc.vector.scalar_tensor_tensor(
-            out=turns[:], in0=phi[:, 0:1].to_broadcast([P, 2]), scalar=1.0 / (2.0 * math.pi), in1=turn_offset[:],
-            op0=ALU.mult, op1=ALU.subtract,
+            out=turns[:], in0=shifted[:], scalar=ROUND_MAGIC, in1=turn_offset[:], op0=ALU.subtract, op1=ALU.add
         )
-        nc.vector.tensor_scalar(
-            out=turns[:], in0=turns[:], scalar1=ROUND_MAGIC, scalar2=ROUND_MAGIC, op0=ALU.add, op1=ALU.subtract
-        )
-        nc.vector.tensor_add(out=turns[:], in0=turns[:], in1=turn_offset[:])
         neg_dir = keep.tile([P, 2], F32)
         nc.scalar.activation(out=neg_dir[:], in_=turns[:], func=ACT.Sin, scale=-2.0 * math.pi, bias=phi[:, 0:1])
 
@@ -201,7 +211,7 @@ def tile_polnormal_nolayer_s_kernel(tc, x, coords_x, coords_y, phis, dists_param
 
         def pad_sums(chunk):
             padded = work.tile([P, N_SIGMA], F32)
-            nc.vector.tensor_scalar_add(out=padded[:], in0=gauss_sum[chunk][:], scalar1=SUM_EPS)
+            nc.gpsimd.tensor_scalar_add(out=padded[:], in0=gauss_sum[chunk][:], scalar1=SUM_EPS)
             padded_sum[chunk] = padded
 
         def invert_sums(chunk):
@@ -255,10 +265,10 @@ def tile_polnormal_nolayer_s_kernel(tc, x, coords_x, coords_y, phis, dists_param
         def store(o):
             result = work.tile([P, BATCH, PER_PARTITION, CHANNELS], F32)
             by_batch = products[o][:].rearrange("j r (b c) -> j b r c", b=BATCH)
-            if o % 2 == 0:
-                nc.scalar.copy(out=result[:], in_=by_batch)
-            else:
+            if o < NODES - SCALAR_STORES:
                 nc.vector.tensor_copy(out=result[:], in_=by_batch)
+            else:
+                nc.scalar.copy(out=result[:], in_=by_batch)
             nc.sync.dma_start(
                 out=out_rows[:, o, :].rearrange("b (j f) -> j b f", j=P),
                 in_=result[:].rearrange("j b r c -> j b (r c)"),

@@ -6,9 +6,9 @@ from concourse.masks import make_identity
 
 F32 = mybir.dt.float32
 BF16 = mybir.dt.bfloat16
+I32 = mybir.dt.int32
 U32 = mybir.dt.uint32
 U8 = mybir.dt.uint8
-I32 = mybir.dt.int32
 FP8X4 = mybir.dt.float8_e4m3fn_x4
 ACT = mybir.ActivationFunctionType
 ALU = mybir.AluOpType
@@ -16,23 +16,27 @@ AXIS_X = mybir.AxisListType.X
 
 P = 128
 PACK = 4
+PAIRS = PACK // 2
 BATCH, NODES, CELLS, CHANNELS = 4, 6, 512, 32
 N_PHI, N_DIST, N_SIGMA = 16, 16, 2
+AXES = 2
 HALVES = 2
 DIST_PER_HALF = N_DIST // HALVES
 CHUNKS = NODES * HALVES
-BLOCKS_PER_NODE = CELLS // P
-BLOCKS = NODES * BLOCKS_PER_NODE
-Y_ROW = 32
 COLS = BATCH * CHANNELS
 PER_PARTITION = HALVES * N_SIGMA
 WORDS = CELLS // 2
+ROWS_PER_NODE = CELLS // P
+ROWS = NODES * ROWS_PER_NODE
+Y_ROW = 32
 DIST_UNIT = 2.0
 MIN_SIGMA = 1e-10
 SUM_EPS = 1e-20
-SCALAR_STORES = 2
-X_FIRST = 4
+LOG_SUM_EPS = -46.051701859880914
 ROUND_MAGIC = 12582912.0
+X_FIRST = 4
+SCALAR_STORES = 2
+DEPTH = 3
 
 FLOPS = 2 * NODES * CELLS * (N_PHI * N_DIST * N_SIGMA) * COLS
 
@@ -41,10 +45,10 @@ def tile_polnormal_nolayer_s_kernel(tc, x, coords_x, coords_y, phis, dists_param
     nc = tc.nc
     with ExitStack() as ctx:
         keep = ctx.enter_context(tc.tile_pool(name="keep", bufs=1))
-        work = ctx.enter_context(tc.tile_pool(name="work", bufs=3))
-        psum_flip = ctx.enter_context(tc.psum_pool(name="psum_flip", bufs=3))
-        psum_out = ctx.enter_context(tc.psum_pool(name="psum_out", bufs=2))
-        psum_table = ctx.enter_context(tc.psum_pool(name="psum_table", bufs=2))
+        work = ctx.enter_context(tc.tile_pool(name="work", bufs=DEPTH))
+        psum_turned = ctx.enter_context(tc.psum_pool(name="psum_turned", bufs=DEPTH))
+        psum_products = ctx.enter_context(tc.psum_pool(name="psum_products", bufs=2))
+        psum_positions = ctx.enter_context(tc.psum_pool(name="psum_positions", bufs=2))
         ctx.enter_context(tc.manual_schedule())
 
         phis_all = keep.tile([P, N_PHI], BF16)
@@ -53,15 +57,14 @@ def tile_polnormal_nolayer_s_kernel(tc, x, coords_x, coords_y, phis, dists_param
         nc.sync.dma_start(out=dists_all[:], in_=dists_param.partition_broadcast(P))
         sigma_all = keep.tile([P, N_SIGMA], BF16)
         nc.sync.dma_start(out=sigma_all[:], in_=sigma_param.partition_broadcast(P))
-
-        coord_rows = keep.tile([P, P], BF16)
-        nc.vector.memset(coord_rows[:].bitcast(I32), 0)
+        position_rows = keep.tile([P, P], BF16)
+        nc.vector.memset(position_rows[:].bitcast(I32), 0)
         nc.sync.dma_start(
-            out=coord_rows[0:BLOCKS, :], in_=coords_x.rearrange("a o (kb i) j -> (a o kb) (i j)", kb=BLOCKS_PER_NODE)
+            out=position_rows[0:ROWS, :], in_=coords_x.rearrange("a o (r i) j -> (a o r) (i j)", r=ROWS_PER_NODE)
         )
         nc.sync.dma_start(
-            out=coord_rows[Y_ROW : Y_ROW + BLOCKS, :],
-            in_=coords_y.rearrange("a o (kb i) j -> (a o kb) (i j)", kb=BLOCKS_PER_NODE),
+            out=position_rows[Y_ROW : Y_ROW + ROWS, :],
+            in_=coords_y.rearrange("a o (r i) j -> (a o r) (i j)", r=ROWS_PER_NODE),
         )
         x_raw = keep.tile([P, NODES, BATCH, PACK * CHANNELS], BF16)
         x_cells = x.rearrange("b (o q t) a v c -> o q b (t a v c)", q=P, t=PACK)
@@ -80,16 +83,15 @@ def tile_polnormal_nolayer_s_kernel(tc, x, coords_x, coords_y, phis, dists_param
         nc.vector.tensor_reduce(
             out=pick_dist[:], in_=ident[:].rearrange("j (p r) -> j r p", r=DIST_PER_HALF), axis=AXIS_X, op=ALU.add
         )
-
         pick_turns = keep.tile([P, N_PHI], F32)
         nc.vector.tensor_scalar_mul(out=pick_turns[:], in0=pick_phi[:], scalar1=1.0 / (2.0 * math.pi))
-        turn_offset = keep.tile([P, 2], F32)
+        turn_offset = keep.tile([P, AXES], F32)
         nc.vector.memset(turn_offset[:, 0:1], 0.25)
         nc.vector.memset(turn_offset[:, 1:2], 0.0)
-        neg_turn_offset = keep.tile([P, 2], F32)
+        neg_turn_offset = keep.tile([P, AXES], F32)
         nc.vector.memset(neg_turn_offset[:, 0:1], -0.25)
         nc.vector.memset(neg_turn_offset[:, 1:2], 0.0)
-        to_neg_dir = keep.tile([P, 2], F32)
+        to_neg_dir = keep.tile([P, AXES], F32)
         nc.vector.memset(to_neg_dir[:, 0:1], 0.5 * DIST_UNIT)
         nc.vector.memset(to_neg_dir[:, 1:2], -0.5 * DIST_UNIT)
 
@@ -101,22 +103,22 @@ def tile_polnormal_nolayer_s_kernel(tc, x, coords_x, coords_y, phis, dists_param
         nc.vector.tensor_reduce(out=phi_turns[:], in_=turn_terms[:], axis=AXIS_X, op=ALU.add)
         phi = keep.tile([P, 1], F32)
         nc.vector.tensor_reduce(out=phi[:], in_=phi_terms[:], axis=AXIS_X, op=ALU.add)
-        shifted = keep.tile([P, 2], F32)
+        shifted = keep.tile([P, AXES], F32)
         nc.vector.tensor_scalar(
             out=shifted[:], in0=neg_turn_offset[:], scalar1=phi_turns[:, 0:1], scalar2=ROUND_MAGIC,
             op0=ALU.add, op1=ALU.add,
         )
-        turns = keep.tile([P, 2], F32)
+        turns = keep.tile([P, AXES], F32)
         nc.vector.scalar_tensor_tensor(
             out=turns[:], in0=shifted[:], scalar=ROUND_MAGIC, in1=turn_offset[:], op0=ALU.subtract, op1=ALU.add
         )
-        neg_dir = keep.tile([P, 2], F32)
+        neg_dir = keep.tile([P, AXES], F32)
         nc.scalar.activation(out=neg_dir[:], in_=turns[:], func=ACT.Sin, scale=-2.0 * math.pi, bias=phi[:, 0:1])
 
-        turned = psum_table.tile([P, P], BF16, tag="table")
-        nc.tensor.transpose(out=turned[:], in_=coord_rows[:], identity=ident_bf[:])
-        cell_pos = keep.tile([P, P], BF16)
-        nc.vector.tensor_copy(out=cell_pos[:], in_=turned[:])
+        turned_rows = psum_positions.tile([P, P], BF16, tag="positions")
+        nc.tensor.transpose(out=turned_rows[:], in_=position_rows[:], identity=ident_bf[:])
+        position_cols = keep.tile([P, P], BF16)
+        nc.vector.tensor_copy(out=position_cols[:], in_=turned_rows[:])
 
         dist_terms = keep.tile([P, HALVES, DIST_PER_HALF], F32)
         nc.vector.tensor_mul(
@@ -131,8 +133,8 @@ def tile_polnormal_nolayer_s_kernel(tc, x, coords_x, coords_y, phis, dists_param
         nc.scalar.activation(out=tanh_half[:], in_=logits[:], func=ACT.Tanh, scale=0.5)
         nc.vector.tensor_mul(out=neg_dir[:], in0=neg_dir[:], in1=to_neg_dir[:])
 
-        neg_mu = keep.tile([P, 2, HALVES], F32)
-        for axis in range(2):
+        neg_mu = keep.tile([P, AXES, HALVES], F32)
+        for axis in range(AXES):
             nc.vector.tensor_scalar(
                 out=neg_mu[:, axis, :], in0=tanh_half[:, 0:HALVES], scalar1=1.0, scalar2=neg_dir[:, axis : axis + 1],
                 op0=ALU.add, op1=ALU.mult,
@@ -142,11 +144,21 @@ def tile_polnormal_nolayer_s_kernel(tc, x, coords_x, coords_y, phis, dists_param
             out=sigma[:], in0=tanh_half[:, HALVES:], scalar1=1.0, scalar2=0.5 * DIST_UNIT, op0=ALU.add, op1=ALU.mult
         )
         nc.vector.tensor_scalar_max(out=sigma[:], in0=sigma[:], scalar1=MIN_SIGMA)
-        exp_scale = keep.tile([P, N_SIGMA], F32)
+        neg_two_var = keep.tile([P, N_SIGMA], F32)
         nc.vector.scalar_tensor_tensor(
-            out=exp_scale[:], in0=sigma[:], scalar=-2.0, in1=sigma[:], op0=ALU.mult, op1=ALU.mult
+            out=neg_two_var[:], in0=sigma[:], scalar=-2.0, in1=sigma[:], op0=ALU.mult, op1=ALU.mult
         )
-        nc.vector.reciprocal(out=exp_scale[:], in_=exp_scale[:])
+        exp_scale = keep.tile([P, N_SIGMA], F32)
+        nc.vector.reciprocal(out=exp_scale[:], in_=neg_two_var[:])
+        eps_dist2 = keep.tile([P, N_SIGMA], F32)
+        nc.vector.tensor_scalar_mul(out=eps_dist2[:], in0=neg_two_var[:], scalar1=LOG_SUM_EPS)
+        dist2_ring = keep.tile([P, DEPTH, CELLS + N_SIGMA], F32)
+        nc.vector.tensor_copy(
+            out=dist2_ring[:, :, 0:1], in_=eps_dist2[:, 1:2].unsqueeze(1).to_broadcast([P, DEPTH, 1])
+        )
+        nc.vector.tensor_copy(
+            out=dist2_ring[:, :, CELLS + 1 : CELLS + 2], in_=eps_dist2[:, 0:1].unsqueeze(1).to_broadcast([P, DEPTH, 1])
+        )
 
         x_grouped = keep.tile([P, NODES * BATCH, CHANNELS, PACK], BF16, align_bytes=64)
         x_codes = keep.tile([P, NODES * COLS], U32, align_bytes=64)
@@ -167,74 +179,70 @@ def tile_polnormal_nolayer_s_kernel(tc, x, coords_x, coords_y, phis, dists_param
                 in_=x_grouped[:, rows].rearrange("q n c t -> q (n c t)"),
             )
 
-        tables, squared, dist2, gauss, gauss_sum, padded_sum, inv_sum, flipped, grouped, products = (
-            {}, {}, {}, {}, {}, {}, {}, {}, {}, {},
-        )
+        positions, squared, gauss, gauss_sum, inv_sum, turned, grouped, products = ({}, {}, {}, {}, {}, {}, {}, {})
         out_rows = out.rearrange("b o a p d s c -> b o (a p d s c)")
 
         def spread(o):
-            table = psum_table.tile([P, 2, CELLS], BF16, tag="table")
-            for axis in range(2):
-                for kb in range(BLOCKS_PER_NODE):
-                    row = axis * Y_ROW + o * BLOCKS_PER_NODE + kb
+            table = psum_positions.tile([P, AXES, CELLS], BF16, tag="positions")
+            for axis in range(AXES):
+                for r in range(ROWS_PER_NODE):
+                    row = axis * Y_ROW + o * ROWS_PER_NODE + r
                     nc.tensor.transpose(
-                        out=table[:, axis, kb * P : (kb + 1) * P],
-                        in_=cell_pos[:, row : row + 1].to_broadcast([P, P]),
+                        out=table[:, axis, r * P : (r + 1) * P],
+                        in_=position_cols[:, row : row + 1].to_broadcast([P, P]),
                         identity=ident_bf[:],
                     )
-            tables[o] = table
+            positions[o] = table
 
         def squares(chunk):
             o, h = divmod(chunk, HALVES)
-            sq = work.tile([P, 2, CELLS], F32)
-            for axis in range(2):
+            sq = work.tile([P, AXES, CELLS], F32)
+            for axis in range(AXES):
                 nc.scalar.activation(
-                    out=sq[:, axis, :], in_=tables[o][:, axis, :], func=ACT.Square, bias=neg_mu[:, axis, h : h + 1]
+                    out=sq[:, axis, :], in_=positions[o][:, axis, :], func=ACT.Square, bias=neg_mu[:, axis, h : h + 1]
                 )
             squared[chunk] = sq
 
         def add(chunk):
-            d2 = work.tile([P, CELLS], F32)
-            nc.vector.tensor_add(out=d2[:], in0=squared[chunk][:, 0, :], in1=squared[chunk][:, 1, :])
-            dist2[chunk] = d2
+            nc.vector.tensor_add(
+                out=dist2_ring[:, chunk % DEPTH, 1 : 1 + CELLS], in0=squared[chunk][:, 0, :], in1=squared[chunk][:, 1, :]
+            )
 
         def exps(chunk):
-            g = work.tile([P, N_SIGMA, CELLS], F32)
+            g = work.tile([P, N_SIGMA, CELLS + 1], F32)
             g_sum = work.tile([P, N_SIGMA], F32)
             for s in range(N_SIGMA):
                 nc.scalar.activation(
-                    out=g[:, s, :], in_=dist2[chunk][:], func=ACT.Exp, scale=exp_scale[:, s : s + 1],
+                    out=g[:, s, :],
+                    in_=dist2_ring[:, chunk % DEPTH, 1 - s : 1 - s + CELLS + 1],
+                    func=ACT.Exp,
+                    scale=exp_scale[:, s : s + 1],
                     accum_out=g_sum[:, s : s + 1],
                 )
             gauss[chunk] = g
             gauss_sum[chunk] = g_sum
 
-        def pad_sums(chunk):
-            padded = work.tile([P, N_SIGMA], F32)
-            nc.gpsimd.tensor_scalar_add(out=padded[:], in0=gauss_sum[chunk][:], scalar1=SUM_EPS)
-            padded_sum[chunk] = padded
-
         def invert_sums(chunk):
             inv = work.tile([P, N_SIGMA], F32)
-            nc.vector.reciprocal(out=inv[:], in_=padded_sum[chunk][:])
+            nc.vector.reciprocal(out=inv[:], in_=gauss_sum[chunk][:])
             inv_sum[chunk] = inv
 
-        def normalise_and_flip(chunk):
+        def normalise_and_turn(chunk):
             weights = work.tile([P, N_SIGMA, CELLS], BF16)
             for s in range(N_SIGMA):
                 nc.vector.tensor_scalar_mul(
-                    out=weights[:, s, :], in0=gauss[chunk][:, s, :], scalar1=inv_sum[chunk][:, s : s + 1]
+                    out=weights[:, s, :], in0=gauss[chunk][:, s, s : s + CELLS], scalar1=inv_sum[chunk][:, s : s + 1]
                 )
             words = weights[:].bitcast(F32)
-            flip = psum_flip.tile([P, N_SIGMA, 2, P], F32)
+            planes = psum_turned.tile([P, N_SIGMA, PAIRS, P], F32)
             for s in range(N_SIGMA):
-                for u in range(2):
-                    nc.tensor.transpose(out=flip[:, s, u, :], in_=words[:, s, u:WORDS:2], identity=ident[:])
-            flipped[chunk] = flip
+                for u in range(PAIRS):
+                    nc.tensor.transpose(out=planes[:, s, u, :], in_=words[:, s, u:WORDS:PAIRS], identity=ident[:])
+            turned[chunk] = planes
 
         def regroup(chunk):
-            grp = work.tile([P, N_SIGMA, P, 2], F32, align_bytes=64)
-            nc.vector.tensor_copy(out=grp[:], in_=flipped[chunk][:].rearrange("q s u j -> q s j u"))
+            grp = work.tile([P, N_SIGMA, P, PAIRS], F32, align_bytes=64)
+            nc.vector.tensor_copy(out=grp[:], in_=turned[chunk][:].rearrange("q s u j -> q s j u"))
             grouped[chunk] = grp
 
         def quantise_and_multiply(chunk):
@@ -247,7 +255,7 @@ def tile_polnormal_nolayer_s_kernel(tc, x, coords_x, coords_y, phis, dists_param
                 in_=grouped[chunk][:].rearrange("q s j u -> q (s j u)").bitcast(BF16),
             )
             if h == 0:
-                product = psum_out.tile([P, PER_PARTITION, COLS], F32)
+                product = psum_products.tile([P, PER_PARTITION, COLS], F32)
                 products[o] = product
             node_cols = slice(o * COLS, (o + 1) * COLS)
             for s in range(N_SIGMA):
@@ -278,11 +286,8 @@ def tile_polnormal_nolayer_s_kernel(tc, x, coords_x, coords_y, phis, dists_param
         spread(1)
         squares(0)
         squares(1)
-        regroup_x(0, X_FIRST)
         add(0)
-        regroup_x(X_FIRST, NODES - X_FIRST)
-        quantise_x(0, X_FIRST)
-        quantise_x(X_FIRST, NODES - X_FIRST)
+        regroup_x(0, X_FIRST)
         for chunk in range(CHUNKS):
             o, h = divmod(chunk, HALVES)
             if h == 1 and o + 2 < NODES:
@@ -290,15 +295,19 @@ def tile_polnormal_nolayer_s_kernel(tc, x, coords_x, coords_y, phis, dists_param
             exps(chunk)
             if chunk + 2 < CHUNKS:
                 squares(chunk + 2)
-            pad_sums(chunk)
             if chunk + 1 < CHUNKS:
                 add(chunk + 1)
             invert_sums(chunk)
             if chunk >= 1:
                 regroup(chunk - 1)
-            normalise_and_flip(chunk)
+            else:
+                regroup_x(X_FIRST, NODES - X_FIRST)
+            normalise_and_turn(chunk)
             if chunk >= 1:
                 quantise_and_multiply(chunk - 1)
+            else:
+                quantise_x(0, X_FIRST)
+                quantise_x(X_FIRST, NODES - X_FIRST)
             if h == 1 and o >= 1:
                 store(o - 1)
         regroup(CHUNKS - 1)

@@ -21,21 +21,19 @@ BATCH, NODES, CELLS, CHANNELS = 4, 6, 512, 32
 N_PHI, N_DIST, N_SIGMA = 16, 16, 2
 AXES = 2
 HALVES = 2
-DIST_PER_HALF = N_DIST // HALVES
+PHI_PER_HALF = N_PHI // HALVES
 CHUNKS = NODES * HALVES
 COLS = BATCH * CHANNELS
-PER_PARTITION = HALVES * N_SIGMA
 WORDS = CELLS // 2
 ROWS_PER_NODE = CELLS // P
 ROWS = NODES * ROWS_PER_NODE
 Y_ROW = 32
 DIST_UNIT = 2.0
+HALF_UNIT = 0.5 * DIST_UNIT
 MIN_SIGMA = 1e-10
 SUM_EPS = 1e-20
-LOG_SUM_EPS = -46.051701859880914
 ROUND_MAGIC = 12582912.0
 X_FIRST = 4
-SCALAR_STORES = 2
 DEPTH = 3
 
 FLOPS = 2 * NODES * CELLS * (N_PHI * N_DIST * N_SIGMA) * COLS
@@ -46,17 +44,16 @@ def tile_polnormal_nolayer_s_kernel(tc, x, coords_x, coords_y, phis, dists_param
     with ExitStack() as ctx:
         keep = ctx.enter_context(tc.tile_pool(name="keep", bufs=1))
         work = ctx.enter_context(tc.tile_pool(name="work", bufs=DEPTH))
+        psum_z = ctx.enter_context(tc.psum_pool(name="psum_z", bufs=DEPTH))
         psum_turned = ctx.enter_context(tc.psum_pool(name="psum_turned", bufs=DEPTH))
         psum_products = ctx.enter_context(tc.psum_pool(name="psum_products", bufs=2))
-        psum_positions = ctx.enter_context(tc.psum_pool(name="psum_positions", bufs=2))
         ctx.enter_context(tc.manual_schedule())
 
         phis_all = keep.tile([P, N_PHI], BF16)
         nc.sync.dma_start(out=phis_all[:], in_=phis.partition_broadcast(P))
-        dists_all = keep.tile([P, N_DIST], BF16)
-        nc.sync.dma_start(out=dists_all[:], in_=dists_param.partition_broadcast(P))
-        sigma_all = keep.tile([P, N_SIGMA], BF16)
-        nc.sync.dma_start(out=sigma_all[:], in_=sigma_param.partition_broadcast(P))
+        logits = keep.tile([P, 2 * N_DIST], BF16)
+        nc.scalar.dma_start(out=logits[:, 0:N_DIST], in_=dists_param.partition_broadcast(P))
+        nc.scalar.dma_start(out=logits[:, N_DIST : N_DIST + N_SIGMA], in_=sigma_param.partition_broadcast(P))
         position_rows = keep.tile([P, P], BF16)
         nc.vector.memset(position_rows[:].bitcast(I32), 0)
         nc.sync.dma_start(
@@ -71,94 +68,127 @@ def tile_polnormal_nolayer_s_kernel(tc, x, coords_x, coords_y, phis, dists_param
         for o in range(NODES):
             nc.sync.dma_start(out=x_raw[:, o], in_=x_cells[o])
 
+        warm = keep.tile([P, 1], F32)
+        nc.vector.memset(warm[:], 0.0)
+        warm_out = keep.tile([P, 1], F32)
+        nc.scalar.activation(out=warm_out[:], in_=warm[:], func=ACT.Silu)
+
         ident = keep.tile([P, P], F32)
         make_identity(nc, ident[:])
+        turn_offset = keep.tile([P, AXES, N_PHI], F32)
+        nc.vector.memset(turn_offset[:, 0, :], -0.25)
+        nc.vector.memset(turn_offset[:, 1, :], 0.0)
+        neg_turn_offset = keep.tile([P, AXES, N_PHI], F32)
+        nc.vector.memset(neg_turn_offset[:, 0, :], 0.25)
+        nc.vector.memset(neg_turn_offset[:, 1, :], 0.0)
         ident_bf = keep.tile([P, P], BF16)
         nc.vector.tensor_copy(out=ident_bf[:], in_=ident[:])
-        pick_phi = keep.tile([P, N_PHI], F32)
+        pick_dist = keep.tile([P, N_DIST], F32)
         nc.vector.tensor_reduce(
-            out=pick_phi[:], in_=ident[:].rearrange("j (p r) -> j p r", r=DIST_PER_HALF), axis=AXIS_X, op=ALU.add
+            out=pick_dist[:], in_=ident[:].rearrange("j (a d) -> j d a", d=N_DIST), axis=AXIS_X, op=ALU.add
         )
-        pick_dist = keep.tile([P, DIST_PER_HALF], F32)
-        nc.vector.tensor_reduce(
-            out=pick_dist[:], in_=ident[:].rearrange("j (p r) -> j r p", r=DIST_PER_HALF), axis=AXIS_X, op=ALU.add
-        )
-        pick_turns = keep.tile([P, N_PHI], F32)
-        nc.vector.tensor_scalar_mul(out=pick_turns[:], in0=pick_phi[:], scalar1=1.0 / (2.0 * math.pi))
-        turn_offset = keep.tile([P, AXES], F32)
-        nc.vector.memset(turn_offset[:, 0:1], 0.25)
-        nc.vector.memset(turn_offset[:, 1:2], 0.0)
-        neg_turn_offset = keep.tile([P, AXES], F32)
-        nc.vector.memset(neg_turn_offset[:, 0:1], -0.25)
-        nc.vector.memset(neg_turn_offset[:, 1:2], 0.0)
-        to_neg_dir = keep.tile([P, AXES], F32)
-        nc.vector.memset(to_neg_dir[:, 0:1], 0.5 * DIST_UNIT)
-        nc.vector.memset(to_neg_dir[:, 1:2], -0.5 * DIST_UNIT)
 
-        turn_terms = keep.tile([P, N_PHI], F32)
-        nc.vector.tensor_mul(out=turn_terms[:], in0=phis_all[:], in1=pick_turns[:])
-        phi_terms = keep.tile([P, N_PHI], F32)
-        nc.vector.tensor_mul(out=phi_terms[:], in0=phis_all[:], in1=pick_phi[:])
-        phi_turns = keep.tile([P, 1], F32)
-        nc.vector.tensor_reduce(out=phi_turns[:], in_=turn_terms[:], axis=AXIS_X, op=ALU.add)
-        phi = keep.tile([P, 1], F32)
-        nc.vector.tensor_reduce(out=phi[:], in_=phi_terms[:], axis=AXIS_X, op=ALU.add)
-        shifted = keep.tile([P, AXES], F32)
-        nc.vector.tensor_scalar(
-            out=shifted[:], in0=neg_turn_offset[:], scalar1=phi_turns[:, 0:1], scalar2=ROUND_MAGIC,
-            op0=ALU.add, op1=ALU.add,
-        )
-        turns = keep.tile([P, AXES], F32)
+        phis_both = phis_all[:].unsqueeze(1).to_broadcast([P, AXES, N_PHI])
+        shifted_turns = keep.tile([P, AXES, N_PHI], F32)
         nc.vector.scalar_tensor_tensor(
-            out=turns[:], in0=shifted[:], scalar=ROUND_MAGIC, in1=turn_offset[:], op0=ALU.subtract, op1=ALU.add
+            out=shifted_turns[:], in0=phis_both, scalar=1.0 / (2.0 * math.pi), in1=neg_turn_offset[:],
+            op0=ALU.mult, op1=ALU.add,
         )
-        neg_dir = keep.tile([P, AXES], F32)
-        nc.scalar.activation(out=neg_dir[:], in_=turns[:], func=ACT.Sin, scale=-2.0 * math.pi, bias=phi[:, 0:1])
+        rounded = keep.tile([P, AXES, N_PHI], F32)
+        nc.vector.tensor_scalar_add(out=rounded[:], in0=shifted_turns[:], scalar1=ROUND_MAGIC)
+        turns = keep.tile([P, AXES, N_PHI], F32)
+        nc.vector.scalar_tensor_tensor(
+            out=turns[:], in0=rounded[:], scalar=ROUND_MAGIC, in1=turn_offset[:], op0=ALU.subtract, op1=ALU.add
+        )
+        angle = keep.tile([P, AXES, N_PHI], F32)
+        nc.vector.scalar_tensor_tensor(
+            out=angle[:], in0=turns[:], scalar=-2.0 * math.pi, in1=phis_both, op0=ALU.mult, op1=ALU.add
+        )
+        tanh_half = keep.tile([P, N_DIST + N_SIGMA], F32)
+        nc.scalar.activation(out=tanh_half[:], in_=logits[:, 0 : N_DIST + N_SIGMA], func=ACT.Tanh, scale=0.5)
+        direction = keep.tile([P, AXES, N_PHI], F32)
+        nc.scalar.activation(out=direction[:], in_=angle[:], func=ACT.Sin)
 
-        turned_rows = psum_positions.tile([P, P], BF16, tag="positions")
+        turned_rows = psum_z.tile([P, P], BF16, tag="z")
         nc.tensor.transpose(out=turned_rows[:], in_=position_rows[:], identity=ident_bf[:])
-        position_cols = keep.tile([P, P], BF16)
-        nc.vector.tensor_copy(out=position_cols[:], in_=turned_rows[:])
+        by_axis = turned_rows[:, 0 : AXES * Y_ROW].rearrange("q (a m) -> q a m", a=AXES)
+        pos_scaled = keep.tile([P, AXES, Y_ROW], F32)
+        nc.vector.tensor_scalar_mul(out=pos_scaled[:], in0=by_axis, scalar1=DIST_UNIT)
+        pos_squared = keep.tile([P, AXES, Y_ROW], F32)
+        nc.scalar.activation(out=pos_squared[:], in_=by_axis, func=ACT.Square)
+        nc.scalar.activation(out=warm_out[:], in_=warm[:], func=ACT.Exp)
 
-        dist_terms = keep.tile([P, HALVES, DIST_PER_HALF], F32)
-        nc.vector.tensor_mul(
-            out=dist_terms[:],
-            in0=dists_all[:].rearrange("j (r h) -> j h r", h=HALVES),
-            in1=pick_dist[:].unsqueeze(1).to_broadcast([P, HALVES, DIST_PER_HALF]),
-        )
-        logits = keep.tile([P, HALVES + N_SIGMA], F32)
-        nc.vector.tensor_reduce(out=logits[:, 0:HALVES], in_=dist_terms[:], axis=AXIS_X, op=ALU.add)
-        nc.vector.tensor_copy(out=logits[:, HALVES:], in_=sigma_all[:])
-        tanh_half = keep.tile([P, HALVES + N_SIGMA], F32)
-        nc.scalar.activation(out=tanh_half[:], in_=logits[:], func=ACT.Tanh, scale=0.5)
-        nc.vector.tensor_mul(out=neg_dir[:], in0=neg_dir[:], in1=to_neg_dir[:])
-
-        neg_mu = keep.tile([P, AXES, HALVES], F32)
-        for axis in range(AXES):
-            nc.vector.tensor_scalar(
-                out=neg_mu[:, axis, :], in0=tanh_half[:, 0:HALVES], scalar1=1.0, scalar2=neg_dir[:, axis : axis + 1],
-                op0=ALU.add, op1=ALU.mult,
-            )
-        sigma = keep.tile([P, N_SIGMA], F32)
+        one_plus = keep.tile([P, N_DIST + N_SIGMA], F32)
         nc.vector.tensor_scalar(
-            out=sigma[:], in0=tanh_half[:, HALVES:], scalar1=1.0, scalar2=0.5 * DIST_UNIT, op0=ALU.add, op1=ALU.mult
+            out=one_plus[:], in0=tanh_half[:], scalar1=1.0, scalar2=MIN_SIGMA / HALF_UNIT, op0=ALU.add, op1=ALU.max
         )
-        nc.vector.tensor_scalar_max(out=sigma[:], in0=sigma[:], scalar1=MIN_SIGMA)
-        neg_two_var = keep.tile([P, N_SIGMA], F32)
+        inverse = keep.tile([P, N_DIST + N_SIGMA], F32)
+        nc.vector.reciprocal(out=inverse[:], in_=one_plus[:])
+        neg_norm2 = keep.tile([P, Y_ROW], F32)
         nc.vector.scalar_tensor_tensor(
-            out=neg_two_var[:], in0=sigma[:], scalar=-2.0, in1=sigma[:], op0=ALU.mult, op1=ALU.mult
+            out=neg_norm2[:], in0=pos_squared[:, 0, :], scalar=-1.0, in1=pos_squared[:, 1, :],
+            op0=ALU.mult, op1=ALU.subtract,
         )
+
+        proj_terms = keep.tile([P, AXES, ROWS, N_PHI], F32)
+        proj = keep.tile([P, ROWS, N_PHI], F32)
+
+        def project(first, count):
+            n = count * ROWS_PER_NODE
+            rows = slice(first * ROWS_PER_NODE, first * ROWS_PER_NODE + n)
+            nc.vector.tensor_tensor(
+                out=proj_terms[:, :, rows, :],
+                in0=pos_scaled[:, :, rows].unsqueeze(3).to_broadcast([P, AXES, n, N_PHI]),
+                in1=direction[:].unsqueeze(2).to_broadcast([P, AXES, n, N_PHI]),
+                op=ALU.mult,
+            )
+            nc.vector.tensor_add(out=proj[:, rows, :], in0=proj_terms[:, 0, rows, :], in1=proj_terms[:, 1, rows, :])
+
+        z_cells, z_comps, gauss, gauss_sum, padded_sum, inv_sum = ({}, {}, {}, {}, {}, {})
+        turned, grouped, products = ({}, {}, {})
+
+        def new_z_cells(o):
+            zc = work.tile([P, ROWS_PER_NODE, N_PHI, N_DIST], F32)
+            z_cells[o] = zc
+
+        def exponent_rows(o, rows, first_phi, n_phi):
+            for r in rows:
+                row = o * ROWS_PER_NODE + r
+                nc.vector.scalar_tensor_tensor(
+                    out=z_cells[o][:, r, first_phi : first_phi + n_phi, :],
+                    in0=inverse[:, 0:N_DIST].unsqueeze(1).to_broadcast([P, n_phi, N_DIST]),
+                    scalar=neg_norm2[:, row : row + 1],
+                    in1=proj[:, row, first_phi : first_phi + n_phi].unsqueeze(2).to_broadcast([P, n_phi, N_DIST]),
+                    op0=ALU.mult,
+                    op1=ALU.add,
+                )
+
+        def turn_exponents(chunk):
+            o, h = divmod(chunk, HALVES)
+            z = psum_z.tile([P, CELLS], F32, tag="z")
+            flat = z_cells[o][:].rearrange("q r p d -> q r (p d)")
+            for r in range(ROWS_PER_NODE):
+                nc.tensor.transpose(out=z[:, r * P : (r + 1) * P], in_=flat[:, r, h * P : (h + 1) * P], identity=ident[:])
+            z_comps[chunk] = z
+
         exp_scale = keep.tile([P, N_SIGMA], F32)
-        nc.vector.reciprocal(out=exp_scale[:], in_=neg_two_var[:])
-        eps_dist2 = keep.tile([P, N_SIGMA], F32)
-        nc.vector.tensor_scalar_mul(out=eps_dist2[:], in0=neg_two_var[:], scalar1=LOG_SUM_EPS)
-        dist2_ring = keep.tile([P, DEPTH, CELLS + N_SIGMA], F32)
-        nc.vector.tensor_copy(
-            out=dist2_ring[:, :, 0:1], in_=eps_dist2[:, 1:2].unsqueeze(1).to_broadcast([P, DEPTH, 1])
-        )
-        nc.vector.tensor_copy(
-            out=dist2_ring[:, :, CELLS + 1 : CELLS + 2], in_=eps_dist2[:, 0:1].unsqueeze(1).to_broadcast([P, DEPTH, 1])
-        )
+        exp_bias = keep.tile([P, N_SIGMA], F32)
+
+        def scale_and_bias():
+            pick_terms = keep.tile([P, N_DIST], F32)
+            nc.vector.tensor_mul(out=pick_terms[:], in0=one_plus[:, 0:N_DIST], in1=pick_dist[:])
+            own = keep.tile([P, 1], F32)
+            nc.vector.tensor_reduce(out=own[:], in_=pick_terms[:], axis=AXIS_X, op=ALU.add)
+            half_inv_var = keep.tile([P, N_SIGMA], F32)
+            nc.vector.scalar_tensor_tensor(
+                out=half_inv_var[:], in0=inverse[:, N_DIST:], scalar=0.5 / (HALF_UNIT * HALF_UNIT),
+                in1=inverse[:, N_DIST:], op0=ALU.mult, op1=ALU.mult,
+            )
+            nc.vector.tensor_scalar_mul(out=exp_scale[:], in0=half_inv_var[:], scalar1=own[:, 0:1])
+            nc.vector.tensor_scalar(
+                out=exp_bias[:], in0=exp_scale[:], scalar1=own[:, 0:1], scalar2=-HALF_UNIT * HALF_UNIT,
+                op0=ALU.mult, op1=ALU.mult,
+            )
 
         x_grouped = keep.tile([P, NODES * BATCH, CHANNELS, PACK], BF16, align_bytes=64)
         x_codes = keep.tile([P, NODES * COLS], U32, align_bytes=64)
@@ -179,59 +209,36 @@ def tile_polnormal_nolayer_s_kernel(tc, x, coords_x, coords_y, phis, dists_param
                 in_=x_grouped[:, rows].rearrange("q n c t -> q (n c t)"),
             )
 
-        positions, squared, gauss, gauss_sum, inv_sum, turned, grouped, products = ({}, {}, {}, {}, {}, {}, {}, {})
         out_rows = out.rearrange("b o a p d s c -> b o (a p d s c)")
 
-        def spread(o):
-            table = psum_positions.tile([P, AXES, CELLS], BF16, tag="positions")
-            for axis in range(AXES):
-                for r in range(ROWS_PER_NODE):
-                    row = axis * Y_ROW + o * ROWS_PER_NODE + r
-                    nc.tensor.transpose(
-                        out=table[:, axis, r * P : (r + 1) * P],
-                        in_=position_cols[:, row : row + 1].to_broadcast([P, P]),
-                        identity=ident_bf[:],
-                    )
-            positions[o] = table
-
-        def squares(chunk):
-            o, h = divmod(chunk, HALVES)
-            sq = work.tile([P, AXES, CELLS], F32)
-            for axis in range(AXES):
-                nc.scalar.activation(
-                    out=sq[:, axis, :], in_=positions[o][:, axis, :], func=ACT.Square, bias=neg_mu[:, axis, h : h + 1]
-                )
-            squared[chunk] = sq
-
-        def add(chunk):
-            nc.vector.tensor_add(
-                out=dist2_ring[:, chunk % DEPTH, 1 : 1 + CELLS], in0=squared[chunk][:, 0, :], in1=squared[chunk][:, 1, :]
-            )
-
         def exps(chunk):
-            g = work.tile([P, N_SIGMA, CELLS + 1], F32)
+            g = work.tile([P, N_SIGMA, CELLS], F32)
             g_sum = work.tile([P, N_SIGMA], F32)
             for s in range(N_SIGMA):
                 nc.scalar.activation(
                     out=g[:, s, :],
-                    in_=dist2_ring[:, chunk % DEPTH, 1 - s : 1 - s + CELLS + 1],
+                    in_=z_comps[chunk][:],
                     func=ACT.Exp,
                     scale=exp_scale[:, s : s + 1],
+                    bias=exp_bias[:, s : s + 1],
                     accum_out=g_sum[:, s : s + 1],
                 )
             gauss[chunk] = g
             gauss_sum[chunk] = g_sum
+            padded = work.tile([P, N_SIGMA], F32)
+            nc.gpsimd.tensor_scalar_add(out=padded[:], in0=g_sum[:], scalar1=SUM_EPS)
+            padded_sum[chunk] = padded
 
         def invert_sums(chunk):
             inv = work.tile([P, N_SIGMA], F32)
-            nc.vector.reciprocal(out=inv[:], in_=gauss_sum[chunk][:])
+            nc.vector.reciprocal(out=inv[:], in_=padded_sum[chunk][:])
             inv_sum[chunk] = inv
 
         def normalise_and_turn(chunk):
             weights = work.tile([P, N_SIGMA, CELLS], BF16)
             for s in range(N_SIGMA):
                 nc.vector.tensor_scalar_mul(
-                    out=weights[:, s, :], in0=gauss[chunk][:, s, s : s + CELLS], scalar1=inv_sum[chunk][:, s : s + 1]
+                    out=weights[:, s, :], in0=gauss[chunk][:, s, :], scalar1=inv_sum[chunk][:, s : s + 1]
                 )
             words = weights[:].bitcast(F32)
             planes = psum_turned.tile([P, N_SIGMA, PAIRS, P], F32)
@@ -242,7 +249,7 @@ def tile_polnormal_nolayer_s_kernel(tc, x, coords_x, coords_y, phis, dists_param
 
         def regroup(chunk):
             grp = work.tile([P, N_SIGMA, P, PAIRS], F32, align_bytes=64)
-            nc.vector.tensor_copy(out=grp[:], in_=turned[chunk][:].rearrange("q s u j -> q s j u"))
+            nc.scalar.copy(out=grp[:], in_=turned[chunk][:].rearrange("q s u j -> q s j u"))
             grouped[chunk] = grp
 
         def quantise_and_multiply(chunk):
@@ -254,14 +261,13 @@ def tile_polnormal_nolayer_s_kernel(tc, x, coords_x, coords_y, phis, dists_param
                 scales=scales[:],
                 in_=grouped[chunk][:].rearrange("q s j u -> q (s j u)").bitcast(BF16),
             )
-            if h == 0:
-                product = psum_products.tile([P, PER_PARTITION, COLS], F32)
-                products[o] = product
+            product = psum_products.tile([P, CELLS], F32)
+            products[chunk] = product
             node_cols = slice(o * COLS, (o + 1) * COLS)
             for s in range(N_SIGMA):
                 comp_cols = slice(s * P, (s + 1) * P)
                 nc.tensor.matmul_mx(
-                    out=products[o][:, h * N_SIGMA + s, :],
+                    out=product[:, s * COLS : (s + 1) * COLS],
                     lhsT=codes[:, comp_cols].bitcast(FP8X4),
                     lhsT_scale=scales[:, comp_cols],
                     rhs=x_codes[:, node_cols].bitcast(FP8X4),
@@ -270,46 +276,54 @@ def tile_polnormal_nolayer_s_kernel(tc, x, coords_x, coords_y, phis, dists_param
                     stop=True,
                 )
 
-        def store(o):
-            result = work.tile([P, BATCH, PER_PARTITION, CHANNELS], F32)
-            by_batch = products[o][:].rearrange("j r (b c) -> j b r c", b=BATCH)
-            if o < NODES - SCALAR_STORES:
-                nc.vector.tensor_copy(out=result[:], in_=by_batch)
-            else:
+        def store(chunk):
+            o, h = divmod(chunk, HALVES)
+            result = work.tile([P, BATCH, N_SIGMA, CHANNELS], F32)
+            by_batch = products[chunk][:, 0 : N_SIGMA * COLS].rearrange("j (s b c) -> j b s c", s=N_SIGMA, b=BATCH)
+            if chunk % 2 == 0:
                 nc.scalar.copy(out=result[:], in_=by_batch)
+            else:
+                nc.vector.tensor_copy(out=result[:], in_=by_batch)
+            span = P * N_SIGMA * CHANNELS
             nc.sync.dma_start(
-                out=out_rows[:, o, :].rearrange("b (j f) -> j b f", j=P),
-                in_=result[:].rearrange("j b r c -> j b (r c)"),
+                out=out_rows[:, o, h * span : (h + 1) * span].rearrange("b (j f) -> j b f", j=P),
+                in_=result[:].rearrange("j b s c -> j b (s c)"),
             )
 
-        spread(0)
-        spread(1)
-        squares(0)
-        squares(1)
-        add(0)
-        regroup_x(0, X_FIRST)
-        for chunk in range(CHUNKS):
-            o, h = divmod(chunk, HALVES)
-            if h == 1 and o + 2 < NODES:
-                spread(o + 2)
-            exps(chunk)
-            if chunk + 2 < CHUNKS:
-                squares(chunk + 2)
-            if chunk + 1 < CHUNKS:
-                add(chunk + 1)
-            invert_sums(chunk)
-            if chunk >= 1:
-                regroup(chunk - 1)
-            else:
+        project(0, 1)
+        new_z_cells(0)
+        exponent_rows(0, range(ROWS_PER_NODE), 0, PHI_PER_HALF)
+        turn_exponents(0)
+        scale_and_bias()
+        exponent_rows(0, range(ROWS_PER_NODE), PHI_PER_HALF, PHI_PER_HALF)
+        project(1, NODES - 1)
+        new_z_cells(1)
+        exponent_rows(1, (0, 1), 0, N_PHI)
+        for i in range(CHUNKS + 4):
+            if i + 1 < CHUNKS:
+                turn_exponents(i + 1)
+            if i < CHUNKS:
+                exps(i)
+            if 1 <= i <= CHUNKS:
+                invert_sums(i - 1)
+                normalise_and_turn(i - 1)
+            node = (i + 3) // 2
+            if node < NODES:
+                if i % 2 == 1:
+                    new_z_cells(node)
+                    exponent_rows(node, (0, 1), 0, N_PHI)
+                else:
+                    exponent_rows(node, (2, 3), 0, N_PHI)
+            if 2 <= i < CHUNKS + 2:
+                regroup(i - 2)
+            if i == 0:
+                regroup_x(0, X_FIRST)
+            if i == 1:
                 regroup_x(X_FIRST, NODES - X_FIRST)
-            normalise_and_turn(chunk)
-            if chunk >= 1:
-                quantise_and_multiply(chunk - 1)
-            else:
+            if i == 2:
                 quantise_x(0, X_FIRST)
                 quantise_x(X_FIRST, NODES - X_FIRST)
-            if h == 1 and o >= 1:
-                store(o - 1)
-        regroup(CHUNKS - 1)
-        quantise_and_multiply(CHUNKS - 1)
-        store(NODES - 1)
+            if 3 <= i < CHUNKS + 3:
+                quantise_and_multiply(i - 3)
+            if 4 <= i < CHUNKS + 4:
+                store(i - 4)

@@ -27,7 +27,8 @@ COLS = BATCH * CHANNELS
 WORDS = CELLS // 2
 ROWS_PER_NODE = CELLS // P
 ROWS = NODES * ROWS_PER_NODE
-Y_ROW = 32
+POS_ROWS = 8
+POS_BLOCKS = ROWS // POS_ROWS
 DIST_UNIT = 2.0
 HALF_UNIT = 0.5 * DIST_UNIT
 MIN_SIGMA = 1e-10
@@ -54,14 +55,15 @@ def tile_polnormal_nolayer_s_kernel(tc, x, coords_x, coords_y, phis, dists_param
         logits = keep.tile([P, 2 * N_DIST], BF16)
         nc.scalar.dma_start(out=logits[:, 0:N_DIST], in_=dists_param.partition_broadcast(P))
         nc.scalar.dma_start(out=logits[:, N_DIST : N_DIST + N_SIGMA], in_=sigma_param.partition_broadcast(P))
-        position_rows = keep.tile([P, P], BF16)
-        nc.vector.memset(position_rows[:].bitcast(I32), 0)
+        position_rows = keep.tile([P, POS_BLOCKS * P], BF16)
+        nc.gpsimd.memset(position_rows[:].bitcast(F32), 0.0)
         nc.sync.dma_start(
-            out=position_rows[0:ROWS, :], in_=coords_x.rearrange("a o (r i) j -> (a o r) (i j)", r=ROWS_PER_NODE)
+            out=position_rows[0:POS_ROWS, :],
+            in_=coords_x.rearrange("a o i j -> (a o i j)").rearrange("(m n) -> m n", m=POS_ROWS),
         )
         nc.sync.dma_start(
-            out=position_rows[Y_ROW : Y_ROW + ROWS, :],
-            in_=coords_y.rearrange("a o (r i) j -> (a o r) (i j)", r=ROWS_PER_NODE),
+            out=position_rows[POS_ROWS : AXES * POS_ROWS, :],
+            in_=coords_y.rearrange("a o i j -> (a o i j)").rearrange("(m n) -> m n", m=POS_ROWS),
         )
         x_raw = keep.tile([P, NODES, BATCH, PACK * CHANNELS], BF16)
         x_cells = x.rearrange("b (o q t) a v c -> o q b (t a v c)", q=P, t=PACK)
@@ -109,13 +111,20 @@ def tile_polnormal_nolayer_s_kernel(tc, x, coords_x, coords_y, phis, dists_param
         direction = keep.tile([P, AXES, N_PHI], F32)
         nc.scalar.activation(out=direction[:], in_=angle[:], func=ACT.Sin)
 
-        turned_rows = psum_z.tile([P, P], BF16, tag="z")
-        nc.tensor.transpose(out=turned_rows[:], in_=position_rows[:], identity=ident_bf[:])
-        by_axis = turned_rows[:, 0 : AXES * Y_ROW].rearrange("q (a m) -> q a m", a=AXES)
-        pos_scaled = keep.tile([P, AXES, Y_ROW], F32)
-        nc.vector.tensor_scalar_mul(out=pos_scaled[:], in0=by_axis, scalar1=DIST_UNIT)
-        pos_squared = keep.tile([P, AXES, Y_ROW], F32)
-        nc.scalar.activation(out=pos_squared[:], in_=by_axis, func=ACT.Square)
+        turned_rows = psum_z.tile([P, POS_BLOCKS, P], BF16, tag="z")
+        for b in range(POS_BLOCKS):
+            nc.tensor.transpose(
+                out=turned_rows[:, b, :], in_=position_rows[:, b * P : (b + 1) * P], identity=ident_bf[:]
+            )
+        by_axis = turned_rows[:, :, 0 : AXES * POS_ROWS].rearrange("q b (a m) -> q a m b", a=AXES)
+        pos_scaled = keep.tile([P, AXES, ROWS], F32)
+        nc.vector.tensor_scalar_mul(
+            out=pos_scaled[:].rearrange("q a (m b) -> q a m b", b=POS_BLOCKS), in0=by_axis, scalar1=DIST_UNIT
+        )
+        pos_squared = keep.tile([P, AXES, ROWS], F32)
+        nc.scalar.activation(
+            out=pos_squared[:].rearrange("q a (m b) -> q a m b", b=POS_BLOCKS), in_=by_axis, func=ACT.Square
+        )
         nc.scalar.activation(out=warm_out[:], in_=warm[:], func=ACT.Exp)
 
         one_plus = keep.tile([P, N_DIST + N_SIGMA], F32)
@@ -124,7 +133,7 @@ def tile_polnormal_nolayer_s_kernel(tc, x, coords_x, coords_y, phis, dists_param
         )
         inverse = keep.tile([P, N_DIST + N_SIGMA], F32)
         nc.vector.reciprocal(out=inverse[:], in_=one_plus[:])
-        neg_norm2 = keep.tile([P, Y_ROW], F32)
+        neg_norm2 = keep.tile([P, ROWS], F32)
         nc.vector.scalar_tensor_tensor(
             out=neg_norm2[:], in0=pos_squared[:, 0, :], scalar=-1.0, in1=pos_squared[:, 1, :],
             op0=ALU.mult, op1=ALU.subtract,

@@ -45,6 +45,7 @@ def tile_polnormal_nolayer_s_kernel(tc, x, coords_x, coords_y, phis, dists_param
     with ExitStack() as ctx:
         keep = ctx.enter_context(tc.tile_pool(name="keep", bufs=1))
         work = ctx.enter_context(tc.tile_pool(name="work", bufs=DEPTH))
+        outgoing = ctx.enter_context(tc.tile_pool(name="outgoing", bufs=6))
         psum_z = ctx.enter_context(tc.psum_pool(name="psum_z", bufs=DEPTH))
         psum_turned = ctx.enter_context(tc.psum_pool(name="psum_turned", bufs=DEPTH))
         psum_products = ctx.enter_context(tc.psum_pool(name="psum_products", bufs=2))
@@ -52,9 +53,6 @@ def tile_polnormal_nolayer_s_kernel(tc, x, coords_x, coords_y, phis, dists_param
 
         phis_all = keep.tile([P, N_PHI], BF16)
         nc.sync.dma_start(out=phis_all[:], in_=phis.partition_broadcast(P))
-        logits = keep.tile([P, 2 * N_DIST], BF16)
-        nc.scalar.dma_start(out=logits[:, 0:N_DIST], in_=dists_param.partition_broadcast(P))
-        nc.scalar.dma_start(out=logits[:, N_DIST : N_DIST + N_SIGMA], in_=sigma_param.partition_broadcast(P))
         position_rows = keep.tile([P, POS_BLOCKS * P], BF16)
         nc.gpsimd.memset(position_rows[:].bitcast(F32), 0.0)
         nc.sync.dma_start(
@@ -65,6 +63,9 @@ def tile_polnormal_nolayer_s_kernel(tc, x, coords_x, coords_y, phis, dists_param
             out=position_rows[POS_ROWS : AXES * POS_ROWS, :],
             in_=coords_y.rearrange("a o i j -> (a o i j)").rearrange("(m n) -> m n", m=POS_ROWS),
         )
+        logits = keep.tile([P, 2 * N_DIST], BF16)
+        nc.sync.dma_start(out=logits[:, 0:N_DIST], in_=dists_param.partition_broadcast(P))
+        nc.sync.dma_start(out=logits[:, N_DIST : N_DIST + N_SIGMA], in_=sigma_param.partition_broadcast(P))
         x_raw = keep.tile([P, NODES, BATCH, PACK * CHANNELS], BF16)
         x_cells = x.rearrange("b (o q t) a v c -> o q b (t a v c)", q=P, t=PACK)
         for o in range(NODES):
@@ -102,57 +103,84 @@ def tile_polnormal_nolayer_s_kernel(tc, x, coords_x, coords_y, phis, dists_param
         nc.vector.scalar_tensor_tensor(
             out=turns[:], in0=rounded[:], scalar=ROUND_MAGIC, in1=turn_offset[:], op0=ALU.subtract, op1=ALU.add
         )
+        tanh_half = keep.tile([P, N_DIST + N_SIGMA], F32)
+        nc.scalar.activation(out=tanh_half[:], in_=logits[:, 0 : N_DIST + N_SIGMA], func=ACT.Tanh, scale=0.5)
+        one_plus = keep.tile([P, N_DIST + N_SIGMA], F32)
+        nc.vector.tensor_scalar(
+            out=one_plus[:], in0=tanh_half[:], scalar1=1.0, scalar2=MIN_SIGMA / HALF_UNIT, op0=ALU.add, op1=ALU.max
+        )
         angle = keep.tile([P, AXES, N_PHI], F32)
         nc.vector.scalar_tensor_tensor(
             out=angle[:], in0=turns[:], scalar=-2.0 * math.pi, in1=phis_both, op0=ALU.mult, op1=ALU.add
         )
-        tanh_half = keep.tile([P, N_DIST + N_SIGMA], F32)
-        nc.scalar.activation(out=tanh_half[:], in_=logits[:, 0 : N_DIST + N_SIGMA], func=ACT.Tanh, scale=0.5)
-        direction = keep.tile([P, AXES, N_PHI], F32)
-        nc.scalar.activation(out=direction[:], in_=angle[:], func=ACT.Sin)
-
         turned_rows = psum_z.tile([P, POS_BLOCKS, P], BF16, tag="z")
         for b in range(POS_BLOCKS):
             nc.tensor.transpose(
                 out=turned_rows[:, b, :], in_=position_rows[:, b * P : (b + 1) * P], identity=ident_bf[:]
             )
         by_axis = turned_rows[:, :, 0 : AXES * POS_ROWS].rearrange("q b (a m) -> q a m b", a=AXES)
-        pos_scaled = keep.tile([P, AXES, ROWS], F32)
-        nc.vector.tensor_scalar_mul(
-            out=pos_scaled[:].rearrange("q a (m b) -> q a m b", b=POS_BLOCKS), in0=by_axis, scalar1=DIST_UNIT
-        )
         pos_squared = keep.tile([P, AXES, ROWS], F32)
         nc.scalar.activation(
             out=pos_squared[:].rearrange("q a (m b) -> q a m b", b=POS_BLOCKS), in_=by_axis, func=ACT.Square
         )
+        direction = keep.tile([P, AXES, N_PHI], F32)
+        nc.scalar.activation(out=direction[:], in_=angle[:], func=ACT.Sin)
         nc.scalar.activation(out=warm_out[:], in_=warm[:], func=ACT.Exp)
-
-        one_plus = keep.tile([P, N_DIST + N_SIGMA], F32)
-        nc.vector.tensor_scalar(
-            out=one_plus[:], in0=tanh_half[:], scalar1=1.0, scalar2=MIN_SIGMA / HALF_UNIT, op0=ALU.add, op1=ALU.max
+        pos_scaled = keep.tile([P, AXES, ROWS], F32)
+        nc.vector.tensor_scalar_mul(
+            out=pos_scaled[:].rearrange("q a (m b) -> q a m b", b=POS_BLOCKS), in0=by_axis, scalar1=DIST_UNIT
         )
         inverse = keep.tile([P, N_DIST + N_SIGMA], F32)
         nc.vector.reciprocal(out=inverse[:], in_=one_plus[:])
+        pick_terms = keep.tile([P, N_DIST], F32)
+        nc.vector.tensor_mul(out=pick_terms[:], in0=one_plus[:, 0:N_DIST], in1=pick_dist[:])
         neg_norm2 = keep.tile([P, ROWS], F32)
         nc.vector.scalar_tensor_tensor(
             out=neg_norm2[:], in0=pos_squared[:, 0, :], scalar=-1.0, in1=pos_squared[:, 1, :],
             op0=ALU.mult, op1=ALU.subtract,
         )
+        own = keep.tile([P, 1], F32)
+        half_inv_var = keep.tile([P, N_SIGMA], F32)
+
+        def make_own():
+            nc.vector.tensor_reduce(out=own[:], in_=pick_terms[:], axis=AXIS_X, op=ALU.add)
+
+        def make_half_inv_var():
+            nc.vector.scalar_tensor_tensor(
+                out=half_inv_var[:], in0=inverse[:, N_DIST:], scalar=0.5 / (HALF_UNIT * HALF_UNIT),
+                in1=inverse[:, N_DIST:], op0=ALU.mult, op1=ALU.mult,
+            )
 
         proj_terms = keep.tile([P, AXES, ROWS, N_PHI], F32)
         proj = keep.tile([P, ROWS, N_PHI], F32)
+        radial = keep.tile([P, ROWS, N_DIST], F32)
 
-        def project(first, count):
-            n = count * ROWS_PER_NODE
-            rows = slice(first * ROWS_PER_NODE, first * ROWS_PER_NODE + n)
+        def rows_of(first, count):
+            return slice(first * ROWS_PER_NODE, (first + count) * ROWS_PER_NODE), count * ROWS_PER_NODE
+
+        def project_terms(first, count):
+            rows, n = rows_of(first, count)
             nc.vector.tensor_tensor(
                 out=proj_terms[:, :, rows, :],
                 in0=pos_scaled[:, :, rows].unsqueeze(3).to_broadcast([P, AXES, n, N_PHI]),
                 in1=direction[:].unsqueeze(2).to_broadcast([P, AXES, n, N_PHI]),
                 op=ALU.mult,
             )
+
+        def radial_rows(first, count):
+            rows, n = rows_of(first, count)
+            nc.vector.tensor_tensor(
+                out=radial[:, rows, :],
+                in0=neg_norm2[:, rows].unsqueeze(2).to_broadcast([P, n, N_DIST]),
+                in1=inverse[:, 0:N_DIST].unsqueeze(1).to_broadcast([P, n, N_DIST]),
+                op=ALU.mult,
+            )
+
+        def project_sum(first, count):
+            rows, n = rows_of(first, count)
             nc.vector.tensor_add(out=proj[:, rows, :], in0=proj_terms[:, 0, rows, :], in1=proj_terms[:, 1, rows, :])
 
+        BOTH = (0, 1)
         z_cells, z_comps, gauss, gauss_sum, padded_sum, inv_sum = ({}, {}, {}, {}, {}, {})
         turned, grouped, products = ({}, {}, {})
 
@@ -160,17 +188,14 @@ def tile_polnormal_nolayer_s_kernel(tc, x, coords_x, coords_y, phis, dists_param
             zc = work.tile([P, ROWS_PER_NODE, N_PHI, N_DIST], F32)
             z_cells[o] = zc
 
-        def exponent_rows(o, rows, first_phi, n_phi):
-            for r in rows:
-                row = o * ROWS_PER_NODE + r
-                nc.vector.scalar_tensor_tensor(
-                    out=z_cells[o][:, r, first_phi : first_phi + n_phi, :],
-                    in0=inverse[:, 0:N_DIST].unsqueeze(1).to_broadcast([P, n_phi, N_DIST]),
-                    scalar=neg_norm2[:, row : row + 1],
-                    in1=proj[:, row, first_phi : first_phi + n_phi].unsqueeze(2).to_broadcast([P, n_phi, N_DIST]),
-                    op0=ALU.mult,
-                    op1=ALU.add,
-                )
+        def exponent_rows(o, first_row, n_rows, first_phi, n_phi):
+            rows = slice(o * ROWS_PER_NODE + first_row, o * ROWS_PER_NODE + first_row + n_rows)
+            nc.vector.tensor_tensor(
+                out=z_cells[o][:, first_row : first_row + n_rows, first_phi : first_phi + n_phi, :],
+                in0=radial[:, rows, :].unsqueeze(2).to_broadcast([P, n_rows, n_phi, N_DIST]),
+                in1=proj[:, rows, first_phi : first_phi + n_phi].unsqueeze(3).to_broadcast([P, n_rows, n_phi, N_DIST]),
+                op=ALU.add,
+            )
 
         def turn_exponents(chunk):
             o, h = divmod(chunk, HALVES)
@@ -183,17 +208,10 @@ def tile_polnormal_nolayer_s_kernel(tc, x, coords_x, coords_y, phis, dists_param
         exp_scale = keep.tile([P, N_SIGMA], F32)
         exp_bias = keep.tile([P, N_SIGMA], F32)
 
-        def scale_and_bias():
-            pick_terms = keep.tile([P, N_DIST], F32)
-            nc.vector.tensor_mul(out=pick_terms[:], in0=one_plus[:, 0:N_DIST], in1=pick_dist[:])
-            own = keep.tile([P, 1], F32)
-            nc.vector.tensor_reduce(out=own[:], in_=pick_terms[:], axis=AXIS_X, op=ALU.add)
-            half_inv_var = keep.tile([P, N_SIGMA], F32)
-            nc.vector.scalar_tensor_tensor(
-                out=half_inv_var[:], in0=inverse[:, N_DIST:], scalar=0.5 / (HALF_UNIT * HALF_UNIT),
-                in1=inverse[:, N_DIST:], op0=ALU.mult, op1=ALU.mult,
-            )
+        def make_exp_scale():
             nc.vector.tensor_scalar_mul(out=exp_scale[:], in0=half_inv_var[:], scalar1=own[:, 0:1])
+
+        def make_exp_bias():
             nc.vector.tensor_scalar(
                 out=exp_bias[:], in0=exp_scale[:], scalar1=own[:, 0:1], scalar2=-HALF_UNIT * HALF_UNIT,
                 op0=ALU.mult, op1=ALU.mult,
@@ -220,7 +238,7 @@ def tile_polnormal_nolayer_s_kernel(tc, x, coords_x, coords_y, phis, dists_param
 
         out_rows = out.rearrange("b o a p d s c -> b o (a p d s c)")
 
-        def exps(chunk):
+        def exps(chunk, eps_on_gpsimd=True):
             g = work.tile([P, N_SIGMA, CELLS], F32)
             g_sum = work.tile([P, N_SIGMA], F32)
             for s in range(N_SIGMA):
@@ -235,45 +253,52 @@ def tile_polnormal_nolayer_s_kernel(tc, x, coords_x, coords_y, phis, dists_param
             gauss[chunk] = g
             gauss_sum[chunk] = g_sum
             padded = work.tile([P, N_SIGMA], F32)
-            nc.gpsimd.tensor_scalar_add(out=padded[:], in0=g_sum[:], scalar1=SUM_EPS)
+            if eps_on_gpsimd:
+                nc.gpsimd.tensor_scalar_add(out=padded[:], in0=g_sum[:], scalar1=SUM_EPS)
             padded_sum[chunk] = padded
-
-        def invert_sums(chunk):
             inv = work.tile([P, N_SIGMA], F32)
-            nc.vector.reciprocal(out=inv[:], in_=padded_sum[chunk][:])
             inv_sum[chunk] = inv
 
-        def normalise_and_turn(chunk):
-            weights = work.tile([P, N_SIGMA, CELLS], BF16)
-            for s in range(N_SIGMA):
+        def add_eps(chunk, s):
+            nc.vector.tensor_scalar_add(
+                out=padded_sum[chunk][:, s : s + 1], in0=gauss_sum[chunk][:, s : s + 1], scalar1=SUM_EPS
+            )
+
+        def invert_sums(chunk, sigmas=BOTH):
+            cols = slice(sigmas[0], sigmas[-1] + 1)
+            nc.vector.reciprocal(out=inv_sum[chunk][:, cols], in_=padded_sum[chunk][:, cols])
+
+        def normalise_and_turn(chunk, sigmas=BOTH):
+            weights = work.tile([P, len(sigmas), CELLS], BF16)
+            for a, s in enumerate(sigmas):
                 nc.vector.tensor_scalar_mul(
-                    out=weights[:, s, :], in0=gauss[chunk][:, s, :], scalar1=inv_sum[chunk][:, s : s + 1]
+                    out=weights[:, a, :], in0=gauss[chunk][:, s, :], scalar1=inv_sum[chunk][:, s : s + 1]
                 )
             words = weights[:].bitcast(F32)
-            planes = psum_turned.tile([P, N_SIGMA, PAIRS, P], F32)
-            for s in range(N_SIGMA):
+            planes = psum_turned.tile([P, len(sigmas), PAIRS, P], F32)
+            for a in range(len(sigmas)):
                 for u in range(PAIRS):
-                    nc.tensor.transpose(out=planes[:, s, u, :], in_=words[:, s, u:WORDS:PAIRS], identity=ident[:])
-            turned[chunk] = planes
+                    nc.tensor.transpose(out=planes[:, a, u, :], in_=words[:, a, u:WORDS:PAIRS], identity=ident[:])
+            turned[(chunk, sigmas)] = planes
 
-        def regroup(chunk):
-            grp = work.tile([P, N_SIGMA, P, PAIRS], F32, align_bytes=64)
-            nc.scalar.copy(out=grp[:], in_=turned[chunk][:].rearrange("q s u j -> q s j u"))
-            grouped[chunk] = grp
+        def regroup(chunk, sigmas=BOTH):
+            grp = work.tile([P, len(sigmas), P, PAIRS], F32, align_bytes=64)
+            nc.scalar.copy(out=grp[:], in_=turned[(chunk, sigmas)][:].rearrange("q s u j -> q s j u"))
+            grouped[(chunk, sigmas)] = grp
 
-        def quantise_and_multiply(chunk):
+        def quantise_and_multiply(chunk, sigmas=BOTH):
             o, h = divmod(chunk, HALVES)
-            codes = work.tile([P, N_SIGMA * P], U32, align_bytes=64)
-            scales = work.tile([P, N_SIGMA * P], U8, align_bytes=64)
+            codes = work.tile([P, len(sigmas) * P], U32, align_bytes=64)
+            scales = work.tile([P, len(sigmas) * P], U8, align_bytes=64)
             nc.vector.quantize_mx(
                 out=codes[:].bitcast(FP8X4),
                 scales=scales[:],
-                in_=grouped[chunk][:].rearrange("q s j u -> q (s j u)").bitcast(BF16),
+                in_=grouped[(chunk, sigmas)][:].rearrange("q s j u -> q (s j u)").bitcast(BF16),
             )
             product = psum_products.tile([P, CELLS], F32)
-            products[chunk] = product
+            products[(chunk, sigmas)] = product
             node_cols = slice(o * COLS, (o + 1) * COLS)
-            for s in range(N_SIGMA):
+            for s in range(len(sigmas)):
                 comp_cols = slice(s * P, (s + 1) * P)
                 nc.tensor.matmul_mx(
                     out=product[:, s * COLS : (s + 1) * COLS],
@@ -285,54 +310,112 @@ def tile_polnormal_nolayer_s_kernel(tc, x, coords_x, coords_y, phis, dists_param
                     stop=True,
                 )
 
-        def store(chunk):
+        def store(chunk, sigmas=BOTH, on_scalar=None):
             o, h = divmod(chunk, HALVES)
-            result = work.tile([P, BATCH, N_SIGMA, CHANNELS], F32)
-            by_batch = products[chunk][:, 0 : N_SIGMA * COLS].rearrange("j (s b c) -> j b s c", s=N_SIGMA, b=BATCH)
-            if chunk % 2 == 0:
+            n = len(sigmas)
+            result = outgoing.tile([P, BATCH, n, CHANNELS], F32)
+            by_batch = products[(chunk, sigmas)][:, 0 : n * COLS].rearrange("j (s b c) -> j b s c", s=n, b=BATCH)
+            if (chunk % 2 == 0) if on_scalar is None else on_scalar:
                 nc.scalar.copy(out=result[:], in_=by_batch)
             else:
                 nc.vector.tensor_copy(out=result[:], in_=by_batch)
             span = P * N_SIGMA * CHANNELS
-            nc.sync.dma_start(
-                out=out_rows[:, o, h * span : (h + 1) * span].rearrange("b (j f) -> j b f", j=P),
-                in_=result[:].rearrange("j b s c -> j b (s c)"),
-            )
+            half_rows = out_rows[:, o, h * span : (h + 1) * span]
+            if n == N_SIGMA:
+                nc.sync.dma_start(
+                    out=half_rows.rearrange("b (j f) -> j b f", j=P), in_=result[:].rearrange("j b s c -> j b (s c)")
+                )
+            else:
+                nc.sync.dma_start(
+                    out=half_rows.rearrange("b (j s c) -> j b s c", j=P, s=N_SIGMA)[:, :, sigmas[0], :],
+                    in_=result[:, :, 0, :],
+                )
 
-        project(0, 1)
+        project_terms(0, 1)
+        make_own()
+        make_half_inv_var()
+        radial_rows(0, 1)
+        project_sum(0, 1)
+        make_exp_scale()
         new_z_cells(0)
-        exponent_rows(0, range(ROWS_PER_NODE), 0, PHI_PER_HALF)
+        project_terms(1, 1)
+        for r in range(ROWS_PER_NODE):
+            exponent_rows(0, r, 1, 0, PHI_PER_HALF)
         turn_exponents(0)
-        scale_and_bias()
-        exponent_rows(0, range(ROWS_PER_NODE), PHI_PER_HALF, PHI_PER_HALF)
-        project(1, NODES - 1)
+        make_exp_bias()
+        exponent_rows(0, 0, 2, PHI_PER_HALF, PHI_PER_HALF)
+        radial_rows(1, 1)
+        project_sum(1, 1)
+        exponent_rows(0, 2, 2, PHI_PER_HALF, PHI_PER_HALF)
         new_z_cells(1)
-        exponent_rows(1, (0, 1), 0, N_PHI)
-        for i in range(CHUNKS + 4):
+        exponent_rows(1, 0, 2, 0, N_PHI)
+
+        def z_part(i):
+            node = (i + 3) // 2
+            if i % 2 == 1:
+                new_z_cells(node)
+                exponent_rows(node, 0, 2, 0, N_PHI)
+            else:
+                exponent_rows(node, 2, 2, 0, N_PHI)
+
+        for i in range(CHUNKS - 1):
+            has_norm = 1 <= i <= CHUNKS
+            has_z = (i + 3) // 2 < NODES
+            has_q = 3 <= i < CHUNKS + 3
             if i + 1 < CHUNKS:
                 turn_exponents(i + 1)
             if i < CHUNKS:
                 exps(i)
-            if 1 <= i <= CHUNKS:
+            if has_norm:
                 invert_sums(i - 1)
+            if i == 1:
+                project_terms(2, NODES - 2)
+            elif has_z:
+                z_part(i)
+            elif has_q:
+                quantise_and_multiply(i - 3)
+            if has_norm:
                 normalise_and_turn(i - 1)
-            node = (i + 3) // 2
-            if node < NODES:
-                if i % 2 == 1:
-                    new_z_cells(node)
-                    exponent_rows(node, (0, 1), 0, N_PHI)
-                else:
-                    exponent_rows(node, (2, 3), 0, N_PHI)
+            if i == 1:
+                radial_rows(2, NODES - 2)
+                project_sum(2, NODES - 2)
+            if i % 2 == 1 and i // 2 < NODES:
+                regroup_x(i // 2, 1)
+            if i % 2 == 0 and 1 <= i // 2 <= NODES:
+                quantise_x(i // 2 - 1, 1)
+            if i == 1:
+                z_part(i)
             if 2 <= i < CHUNKS + 2:
                 regroup(i - 2)
-            if i == 0:
-                regroup_x(0, X_FIRST)
-            if i == 1:
-                regroup_x(X_FIRST, NODES - X_FIRST)
-            if i == 2:
-                quantise_x(0, X_FIRST)
-                quantise_x(X_FIRST, NODES - X_FIRST)
-            if 3 <= i < CHUNKS + 3:
+            if has_q and has_z:
                 quantise_and_multiply(i - 3)
             if 4 <= i < CHUNKS + 4:
                 store(i - 4)
+
+        last = CHUNKS - 1
+        exps(last, eps_on_gpsimd=False)
+        invert_sums(last - 1)
+        quantise_and_multiply(last - 3)
+        normalise_and_turn(last - 1)
+        add_eps(last, 0)
+        regroup_x(NODES - 1, 1)
+        invert_sums(last, (0,))
+        regroup(last - 2)
+        store(last - 4)
+        add_eps(last, 1)
+        normalise_and_turn(last, (0,))
+        invert_sums(last, (1,))
+        quantise_x(NODES - 1, 1)
+        normalise_and_turn(last, (1,))
+        regroup(last - 1)
+        store(last - 3)
+        quantise_and_multiply(last - 2)
+        quantise_and_multiply(last - 1)
+        regroup(last, (0,))
+        store(last - 2)
+        quantise_and_multiply(last, (0,))
+        regroup(last, (1,))
+        store(last - 1)
+        quantise_and_multiply(last, (1,))
+        store(last, (0,), on_scalar=True)
+        store(last, (1,), on_scalar=False)

@@ -78,9 +78,8 @@ def tile_polnormal_nolayer_s_kernel(tc, x, coords_x, coords_y, phis, dists_param
 
         ident = keep.tile([P, P], F32)
         make_identity(nc, ident[:])
-        turn_offset = keep.tile([P, AXES, N_PHI], F32)
-        nc.vector.memset(turn_offset[:, 0, :], -0.25)
-        nc.vector.memset(turn_offset[:, 1, :], 0.0)
+        quarter = keep.tile([P, 1], F32)
+        nc.vector.tensor_scalar(out=quarter[:], in0=warm[:], scalar1=1.0, scalar2=0.5 * math.pi, op0=ALU.add, op1=ALU.mult)
         neg_turn_offset = keep.tile([P, AXES, N_PHI], F32)
         nc.vector.memset(neg_turn_offset[:, 0, :], 0.25)
         nc.vector.memset(neg_turn_offset[:, 1, :], 0.0)
@@ -97,11 +96,13 @@ def tile_polnormal_nolayer_s_kernel(tc, x, coords_x, coords_y, phis, dists_param
             out=shifted_turns[:], in0=phis_both, scalar=1.0 / (2.0 * math.pi), in1=neg_turn_offset[:],
             op0=ALU.mult, op1=ALU.add,
         )
-        rounded = keep.tile([P, AXES, N_PHI], F32)
-        nc.vector.tensor_scalar_add(out=rounded[:], in0=shifted_turns[:], scalar1=ROUND_MAGIC)
-        turns = keep.tile([P, AXES, N_PHI], F32)
+        whole = keep.tile([P, AXES, N_PHI], F32)
+        nc.vector.tensor_scalar(
+            out=whole[:], in0=shifted_turns[:], scalar1=ROUND_MAGIC, scalar2=ROUND_MAGIC, op0=ALU.add, op1=ALU.subtract
+        )
+        angle = keep.tile([P, AXES, N_PHI], F32)
         nc.vector.scalar_tensor_tensor(
-            out=turns[:], in0=rounded[:], scalar=ROUND_MAGIC, in1=turn_offset[:], op0=ALU.subtract, op1=ALU.add
+            out=angle[:], in0=whole[:], scalar=-2.0 * math.pi, in1=phis_both, op0=ALU.mult, op1=ALU.add
         )
         tanh_half = keep.tile([P, N_DIST + N_SIGMA], F32)
         nc.scalar.activation(out=tanh_half[:], in_=logits[:, 0 : N_DIST + N_SIGMA], func=ACT.Tanh, scale=0.5)
@@ -109,10 +110,9 @@ def tile_polnormal_nolayer_s_kernel(tc, x, coords_x, coords_y, phis, dists_param
         nc.vector.tensor_scalar(
             out=one_plus[:], in0=tanh_half[:], scalar1=1.0, scalar2=MIN_SIGMA / HALF_UNIT, op0=ALU.add, op1=ALU.max
         )
-        angle = keep.tile([P, AXES, N_PHI], F32)
-        nc.vector.scalar_tensor_tensor(
-            out=angle[:], in0=turns[:], scalar=-2.0 * math.pi, in1=phis_both, op0=ALU.mult, op1=ALU.add
-        )
+        direction = keep.tile([P, AXES, N_PHI], F32)
+        nc.scalar.activation(out=direction[:, 0, :], in_=angle[:, 0, :], func=ACT.Sin, bias=quarter[:, 0:1])
+        nc.scalar.activation(out=direction[:, 1, :], in_=angle[:, 1, :], func=ACT.Sin)
         turned_rows = psum_z.tile([P, POS_BLOCKS, P], BF16, tag="z")
         for b in range(POS_BLOCKS):
             nc.tensor.transpose(
@@ -123,8 +123,6 @@ def tile_polnormal_nolayer_s_kernel(tc, x, coords_x, coords_y, phis, dists_param
         nc.scalar.activation(
             out=pos_squared[:].rearrange("q a (m b) -> q a m b", b=POS_BLOCKS), in_=by_axis, func=ACT.Square
         )
-        direction = keep.tile([P, AXES, N_PHI], F32)
-        nc.scalar.activation(out=direction[:], in_=angle[:], func=ACT.Sin)
         nc.scalar.activation(out=warm_out[:], in_=warm[:], func=ACT.Exp)
         pos_scaled = keep.tile([P, AXES, ROWS], F32)
         nc.vector.tensor_scalar_mul(
@@ -390,7 +388,7 @@ def tile_polnormal_nolayer_s_kernel(tc, x, coords_x, coords_y, phis, dists_param
             if has_q and has_z:
                 quantise_and_multiply(i - 3)
             if 4 <= i < CHUNKS + 4:
-                store(i - 4)
+                store(i - 4, on_scalar=False)
 
         last = CHUNKS - 1
         exps(last, eps_on_gpsimd=False)

@@ -236,7 +236,7 @@ def tile_polnormal_nolayer_s_kernel(tc, x, coords_x, coords_y, phis, dists_param
 
         out_rows = out.rearrange("b o a p d s c -> b o (a p d s c)")
 
-        def exps(chunk, eps_on_gpsimd=True):
+        def exps(chunk):
             g = work.tile([P, N_SIGMA, CELLS], F32)
             g_sum = work.tile([P, N_SIGMA], F32)
             for s in range(N_SIGMA):
@@ -251,16 +251,13 @@ def tile_polnormal_nolayer_s_kernel(tc, x, coords_x, coords_y, phis, dists_param
             gauss[chunk] = g
             gauss_sum[chunk] = g_sum
             padded = work.tile([P, N_SIGMA], F32)
-            if eps_on_gpsimd:
-                nc.gpsimd.tensor_scalar_add(out=padded[:], in0=g_sum[:], scalar1=SUM_EPS)
             padded_sum[chunk] = padded
             inv = work.tile([P, N_SIGMA], F32)
             inv_sum[chunk] = inv
 
-        def add_eps(chunk, s):
-            nc.vector.tensor_scalar_add(
-                out=padded_sum[chunk][:, s : s + 1], in0=gauss_sum[chunk][:, s : s + 1], scalar1=SUM_EPS
-            )
+        def add_eps(chunk, sigmas=BOTH):
+            cols = slice(sigmas[0], sigmas[-1] + 1)
+            nc.vector.tensor_scalar_add(out=padded_sum[chunk][:, cols], in0=gauss_sum[chunk][:, cols], scalar1=SUM_EPS)
 
         def invert_sums(chunk, sigmas=BOTH):
             cols = slice(sigmas[0], sigmas[-1] + 1)
@@ -357,56 +354,59 @@ def tile_polnormal_nolayer_s_kernel(tc, x, coords_x, coords_y, phis, dists_param
                 exponent_rows(node, 2, 2, 0, N_PHI)
 
         for i in range(CHUNKS - 1):
-            has_norm = 1 <= i <= CHUNKS
             has_z = (i + 3) // 2 < NODES
-            has_q = 3 <= i < CHUNKS + 3
-            if i + 1 < CHUNKS:
-                turn_exponents(i + 1)
-            if i < CHUNKS:
-                exps(i)
-            if has_norm:
-                invert_sums(i - 1)
+            turn_exponents(i + 1)
+            exps(i)
+            if i >= 1:
+                add_eps(i - 1)
             if i == 1:
                 project_terms(2, NODES - 2)
-            elif has_z:
+            if i == 2:
                 z_part(i)
-            elif has_q:
+            if i >= 3:
                 quantise_and_multiply(i - 3)
-            if has_norm:
-                normalise_and_turn(i - 1)
+            if i >= 1:
+                invert_sums(i - 1)
             if i == 1:
                 radial_rows(2, NODES - 2)
-                project_sum(2, NODES - 2)
-            if i % 2 == 1 and i // 2 < NODES:
-                regroup_x(i // 2, 1)
-            if i % 2 == 0 and 1 <= i // 2 <= NODES:
-                quantise_x(i // 2 - 1, 1)
-            if i == 1:
-                z_part(i)
-            if 2 <= i < CHUNKS + 2:
-                regroup(i - 2)
-            if has_q and has_z:
-                quantise_and_multiply(i - 3)
-            if 4 <= i < CHUNKS + 4:
+            if i == 2:
+                quantise_x(0, 1)
+            if i == 3:
+                regroup_x(1, 1)
+            if i >= 4:
                 store(i - 4, on_scalar=False)
+            if i >= 1:
+                normalise_and_turn(i - 1)
+            if i == 1:
+                project_sum(2, NODES - 2)
+                regroup_x(0, 1)
+            if has_z and i != 2:
+                z_part(i)
+            if i % 2 == 1 and i >= 5:
+                regroup_x(i // 2, 1)
+            if i % 2 == 0 and i >= 4:
+                quantise_x(i // 2 - 1, 1)
+            if i >= 2:
+                regroup(i - 2)
 
         last = CHUNKS - 1
-        exps(last, eps_on_gpsimd=False)
-        invert_sums(last - 1)
-        quantise_and_multiply(last - 3)
-        normalise_and_turn(last - 1)
-        add_eps(last, 0)
+        exps(last)
+        add_eps(last - 1)
         regroup_x(NODES - 1, 1)
+        invert_sums(last - 1)
+        store(last - 4, on_scalar=False)
+        normalise_and_turn(last - 1)
+        add_eps(last, (0,))
+        quantise_and_multiply(last - 3)
         invert_sums(last, (0,))
+        quantise_x(NODES - 1, 1)
         regroup(last - 2)
-        store(last - 4)
-        add_eps(last, 1)
+        add_eps(last, (1,))
         normalise_and_turn(last, (0,))
         invert_sums(last, (1,))
-        quantise_x(NODES - 1, 1)
+        store(last - 3, on_scalar=True)
         normalise_and_turn(last, (1,))
         regroup(last - 1)
-        store(last - 3)
         quantise_and_multiply(last - 2)
         quantise_and_multiply(last - 1)
         regroup(last, (0,))

@@ -373,14 +373,17 @@ def tile_polnormal_nolayer_s_kernel(tc, x, coords_x, coords_y, phis, dists_param
                 quantise_x(0, 1)
             if i == 3:
                 regroup_x(1, 1)
-            if i >= 4:
-                store(i - 4, on_scalar=False)
+            z_early = i >= 4 and i % 2 == 0 and has_z
+            if i >= 4 and i % 2 == 1:
+                store(i - 4)
+            if z_early:
+                z_part(i)
             if i >= 1:
                 normalise_and_turn(i - 1)
             if i == 1:
                 project_sum(2, NODES - 2)
                 regroup_x(0, 1)
-            if has_z and i != 2:
+            if has_z and i != 2 and not z_early:
                 z_part(i)
             if i % 2 == 1 and i >= 5:
                 regroup_x(i // 2, 1)
@@ -388,6 +391,8 @@ def tile_polnormal_nolayer_s_kernel(tc, x, coords_x, coords_y, phis, dists_param
                 quantise_x(i // 2 - 1, 1)
             if i >= 2:
                 regroup(i - 2)
+            if i >= 4 and i % 2 == 0:
+                store(i - 4)
 
         last = CHUNKS - 1
         exps(last)

@@ -151,7 +151,6 @@ def tile_polnormal_nolayer_s_kernel(tc, x, coords_x, coords_y, phis, dists_param
 
         proj_terms = keep.tile([P, AXES, ROWS, N_PHI], F32)
         proj = keep.tile([P, ROWS, N_PHI], F32)
-        radial = keep.tile([P, ROWS, N_DIST], F32)
 
         def rows_of(first, count):
             return slice(first * ROWS_PER_NODE, (first + count) * ROWS_PER_NODE), count * ROWS_PER_NODE
@@ -162,15 +161,6 @@ def tile_polnormal_nolayer_s_kernel(tc, x, coords_x, coords_y, phis, dists_param
                 out=proj_terms[:, :, rows, :],
                 in0=pos_scaled[:, :, rows].unsqueeze(3).to_broadcast([P, AXES, n, N_PHI]),
                 in1=direction[:].unsqueeze(2).to_broadcast([P, AXES, n, N_PHI]),
-                op=ALU.mult,
-            )
-
-        def radial_rows(first, count):
-            rows, n = rows_of(first, count)
-            nc.vector.tensor_tensor(
-                out=radial[:, rows, :],
-                in0=neg_norm2[:, rows].unsqueeze(2).to_broadcast([P, n, N_DIST]),
-                in1=inverse[:, 0:N_DIST].unsqueeze(1).to_broadcast([P, n, N_DIST]),
                 op=ALU.mult,
             )
 
@@ -187,13 +177,16 @@ def tile_polnormal_nolayer_s_kernel(tc, x, coords_x, coords_y, phis, dists_param
             z_cells[o] = zc
 
         def exponent_rows(o, first_row, n_rows, first_phi, n_phi):
-            rows = slice(o * ROWS_PER_NODE + first_row, o * ROWS_PER_NODE + first_row + n_rows)
-            nc.vector.tensor_tensor(
-                out=z_cells[o][:, first_row : first_row + n_rows, first_phi : first_phi + n_phi, :],
-                in0=radial[:, rows, :].unsqueeze(2).to_broadcast([P, n_rows, n_phi, N_DIST]),
-                in1=proj[:, rows, first_phi : first_phi + n_phi].unsqueeze(3).to_broadcast([P, n_rows, n_phi, N_DIST]),
-                op=ALU.add,
-            )
+            for r in range(first_row, first_row + n_rows):
+                row = o * ROWS_PER_NODE + r
+                nc.vector.scalar_tensor_tensor(
+                    out=z_cells[o][:, r, first_phi : first_phi + n_phi, :],
+                    in0=inverse[:, 0:N_DIST].unsqueeze(1).to_broadcast([P, n_phi, N_DIST]),
+                    scalar=neg_norm2[:, row : row + 1],
+                    in1=proj[:, row, first_phi : first_phi + n_phi].unsqueeze(2).to_broadcast([P, n_phi, N_DIST]),
+                    op0=ALU.mult,
+                    op1=ALU.add,
+                )
 
         def turn_exponents(chunk):
             o, h = divmod(chunk, HALVES)
@@ -329,7 +322,6 @@ def tile_polnormal_nolayer_s_kernel(tc, x, coords_x, coords_y, phis, dists_param
         project_terms(0, 1)
         make_own()
         make_half_inv_var()
-        radial_rows(0, 1)
         project_sum(0, 1)
         make_exp_scale()
         new_z_cells(0)
@@ -339,7 +331,6 @@ def tile_polnormal_nolayer_s_kernel(tc, x, coords_x, coords_y, phis, dists_param
         turn_exponents(0)
         make_exp_bias()
         exponent_rows(0, 0, 2, PHI_PER_HALF, PHI_PER_HALF)
-        radial_rows(1, 1)
         project_sum(1, 1)
         exponent_rows(0, 2, 2, PHI_PER_HALF, PHI_PER_HALF)
         new_z_cells(1)
@@ -368,7 +359,8 @@ def tile_polnormal_nolayer_s_kernel(tc, x, coords_x, coords_y, phis, dists_param
             if i >= 1:
                 invert_sums(i - 1)
             if i == 1:
-                radial_rows(2, NODES - 2)
+                regroup_x(0, 1)
+                project_sum(2, NODES - 2)
             if i == 2:
                 quantise_x(0, 1)
             if i == 3:
@@ -380,9 +372,6 @@ def tile_polnormal_nolayer_s_kernel(tc, x, coords_x, coords_y, phis, dists_param
                 z_part(i)
             if i >= 1:
                 normalise_and_turn(i - 1)
-            if i == 1:
-                project_sum(2, NODES - 2)
-                regroup_x(0, 1)
             if has_z and i != 2 and not z_early:
                 z_part(i)
             if i % 2 == 1 and i >= 5:

@@ -212,11 +212,13 @@ def tile_polnormal_nolayer_s_kernel(tc, x, coords_x, coords_y, phis, dists_param
         x_codes = keep.tile([P, NODES * COLS], U32, align_bytes=64)
         x_scales = keep.tile([P, NODES * COLS], U8, align_bytes=64)
 
-        def regroup_x(first, count):
+        def regroup_x(first, count, on_scalar=False):
             rows = slice(first * BATCH, (first + count) * BATCH)
-            nc.vector.tensor_copy(
-                out=x_grouped[:, rows], in_=x_raw[:].rearrange("q o b (t c) -> q (o b) c t", t=PACK)[:, rows]
-            )
+            by_column = x_raw[:].rearrange("q o b (t c) -> q (o b) c t", t=PACK)[:, rows]
+            if on_scalar:
+                nc.scalar.copy(out=x_grouped[:, rows], in_=by_column)
+            else:
+                nc.vector.tensor_copy(out=x_grouped[:, rows], in_=by_column)
 
         def quantise_x(first, count):
             rows = slice(first * BATCH, (first + count) * BATCH)
@@ -319,6 +321,7 @@ def tile_polnormal_nolayer_s_kernel(tc, x, coords_x, coords_y, phis, dists_param
                     in_=result[:, :, 0, :],
                 )
 
+        regroup_x(0, 1, on_scalar=True)
         project_terms(0, 1)
         make_own()
         make_half_inv_var()
@@ -359,7 +362,6 @@ def tile_polnormal_nolayer_s_kernel(tc, x, coords_x, coords_y, phis, dists_param
             if i >= 1:
                 invert_sums(i - 1)
             if i == 1:
-                regroup_x(0, 1)
                 project_sum(2, NODES - 2)
             if i == 2:
                 quantise_x(0, 1)

@@ -67,9 +67,12 @@ def tile_polnormal_nolayer_s_kernel(tc, x, coords_x, coords_y, phis, dists_param
         nc.sync.dma_start(out=logits[:, 0:N_DIST], in_=dists_param.partition_broadcast(P))
         nc.sync.dma_start(out=logits[:, N_DIST : N_DIST + N_SIGMA], in_=sigma_param.partition_broadcast(P))
         x_raw = keep.tile([P, NODES, BATCH, PACK * CHANNELS], BF16)
-        x_cells = x.rearrange("b (o q t) a v c -> o q b (t a v c)", q=P, t=PACK)
+        x_cells = x.rearrange("b (o u q e) a v c -> o u q b (e a v c)", u=PAIRS, q=P, e=2)
         for o in range(NODES):
-            nc.sync.dma_start(out=x_raw[:, o], in_=x_cells[o])
+            for u in range(PAIRS):
+                nc.sync.dma_start(
+                    out=x_raw[:, o, :, u * 2 * CHANNELS : (u + 1) * 2 * CHANNELS], in_=x_cells[o, u]
+                )
 
         warm = keep.tile([P, 1], F32)
         nc.vector.memset(warm[:], 0.0)
@@ -268,7 +271,7 @@ def tile_polnormal_nolayer_s_kernel(tc, x, coords_x, coords_y, phis, dists_param
             planes = psum_turned.tile([P, len(sigmas), PAIRS, P], F32)
             for a in range(len(sigmas)):
                 for u in range(PAIRS):
-                    nc.tensor.transpose(out=planes[:, a, u, :], in_=words[:, a, u:WORDS:PAIRS], identity=ident[:])
+                    nc.tensor.transpose(out=planes[:, a, u, :], in_=words[:, a, u * P : (u + 1) * P], identity=ident[:])
             turned[(chunk, sigmas)] = planes
 
         def regroup(chunk, sigmas=BOTH):

from contextlib import ExitStack
import math

import concourse.mybir as mybir
from concourse.masks import make_identity

F32 = mybir.dt.float32
BF16 = mybir.dt.bfloat16
I32 = mybir.dt.int32
U32 = mybir.dt.uint32
U8 = mybir.dt.uint8
FP8X4 = mybir.dt.float8_e4m3fn_x4
ACT = mybir.ActivationFunctionType
ALU = mybir.AluOpType
AXIS_X = mybir.AxisListType.X

P = 128
PACK = 4
PAIRS = PACK // 2
BATCH, NODES, CELLS, CHANNELS = 4, 6, 512, 32
N_PHI, N_DIST, N_SIGMA = 16, 16, 2
AXES = 2
HALVES = 2
PHI_PER_HALF = N_PHI // HALVES
CHUNKS = NODES * HALVES
COLS = BATCH * CHANNELS
WORDS = CELLS // 2
ROWS_PER_NODE = CELLS // P
ROWS = NODES * ROWS_PER_NODE
POS_ROWS = 8
POS_BLOCKS = ROWS // POS_ROWS
DIST_UNIT = 2.0
HALF_UNIT = 0.5 * DIST_UNIT
MIN_SIGMA = 1e-10
SUM_EPS = 1e-20
ROUND_MAGIC = 12582912.0
X_FIRST = 4
DEPTH = 3

FLOPS = 2 * NODES * CELLS * (N_PHI * N_DIST * N_SIGMA) * COLS


def tile_polnormal_nolayer_s_kernel(tc, x, coords_x, coords_y, phis, dists_param, sigma_param, out):
    nc = tc.nc
    with ExitStack() as ctx:
        keep = ctx.enter_context(tc.tile_pool(name="keep", bufs=1))
        work = ctx.enter_context(tc.tile_pool(name="work", bufs=DEPTH))
        outgoing = ctx.enter_context(tc.tile_pool(name="outgoing", bufs=6))
        psum_z = ctx.enter_context(tc.psum_pool(name="psum_z", bufs=DEPTH))
        psum_turned = ctx.enter_context(tc.psum_pool(name="psum_turned", bufs=DEPTH))
        psum_products = ctx.enter_context(tc.psum_pool(name="psum_products", bufs=2))
        ctx.enter_context(tc.manual_schedule())

        phis_all = keep.tile([P, N_PHI], BF16)
        nc.sync.dma_start(out=phis_all[:], in_=phis.partition_broadcast(P))
        position_rows = keep.tile([P, POS_BLOCKS * P], BF16)
        nc.gpsimd.memset(position_rows[:].bitcast(F32), 0.0)
        nc.sync.dma_start(
            out=position_rows[0:POS_ROWS, :],
            in_=coords_x.rearrange("a o i j -> (a o i j)").rearrange("(m n) -> m n", m=POS_ROWS),
        )
        nc.sync.dma_start(
            out=position_rows[POS_ROWS : AXES * POS_ROWS, :],
            in_=coords_y.rearrange("a o i j -> (a o i j)").rearrange("(m n) -> m n", m=POS_ROWS),
        )
        logits = keep.tile([P, 2 * N_DIST], BF16)
        nc.sync.dma_start(out=logits[:, 0:N_DIST], in_=dists_param.partition_broadcast(P))
        nc.sync.dma_start(out=logits[:, N_DIST : N_DIST + N_SIGMA], in_=sigma_param.partition_broadcast(P))
        x_raw = keep.tile([P, NODES, BATCH, PACK * CHANNELS], BF16)
        x_cells = x.rearrange("b (o u q e) a v c -> o u q b (e a v c)", u=PAIRS, q=P, e=2)
        for o in range(NODES):
            for u in range(PAIRS):
                nc.sync.dma_start(
                    out=x_raw[:, o, :, u * 2 * CHANNELS : (u + 1) * 2 * CHANNELS], in_=x_cells[o, u]
                )

        warm = keep.tile([P, 1], F32)
        nc.vector.memset(warm[:], 0.0)
        warm_out = keep.tile([P, 1], F32)
        nc.scalar.activation(out=warm_out[:], in_=warm[:], func=ACT.Silu)

        ident = keep.tile([P, P], F32)
        make_identity(nc, ident[:])
        quarter = keep.tile([P, 1], F32)
        nc.vector.tensor_scalar(out=quarter[:], in0=warm[:], scalar1=1.0, scalar2=0.5 * math.pi, op0=ALU.add, op1=ALU.mult)
        neg_turn_offset = keep.tile([P, AXES, N_PHI], F32)
        nc.vector.memset(neg_turn_offset[:, 0, :], 0.25)
        nc.vector.memset(neg_turn_offset[:, 1, :], 0.0)
        ident_bf = keep.tile([P, P], BF16)
        nc.vector.tensor_copy(out=ident_bf[:], in_=ident[:])
        pick_dist = keep.tile([P, N_DIST], F32)
        nc.vector.tensor_reduce(
            out=pick_dist[:], in_=ident[:].rearrange("j (a d) -> j d a", d=N_DIST), axis=AXIS_X, op=ALU.add
        )

        phis_both = phis_all[:].unsqueeze(1).to_broadcast([P, AXES, N_PHI])
        shifted_turns = keep.tile([P, AXES, N_PHI], F32)
        nc.vector.scalar_tensor_tensor(
            out=shifted_turns[:], in0=phis_both, scalar=1.0 / (2.0 * math.pi), in1=neg_turn_offset[:],
            op0=ALU.mult, op1=ALU.add,
        )
        whole = keep.tile([P, AXES, N_PHI], F32)
        nc.vector.tensor_scalar(
            out=whole[:], in0=shifted_turns[:], scalar1=ROUND_MAGIC, scalar2=ROUND_MAGIC, op0=ALU.add, op1=ALU.subtract
        )
        angle = keep.tile([P, AXES, N_PHI], F32)
        nc.vector.scalar_tensor_tensor(
            out=angle[:], in0=whole[:], scalar=-2.0 * math.pi, in1=phis_both, op0=ALU.mult, op1=ALU.add
        )
        tanh_half = keep.tile([P, N_DIST + N_SIGMA], F32)
        nc.scalar.activation(out=tanh_half[:], in_=logits[:, 0 : N_DIST + N_SIGMA], func=ACT.Tanh, scale=0.5)
        one_plus = keep.tile([P, N_DIST + N_SIGMA], F32)
        nc.vector.tensor_scalar(
            out=one_plus[:], in0=tanh_half[:], scalar1=1.0, scalar2=MIN_SIGMA / HALF_UNIT, op0=ALU.add, op1=ALU.max
        )
        direction = keep.tile([P, AXES, N_PHI], F32)
        nc.scalar.activation(out=direction[:, 0, :], in_=angle[:, 0, :], func=ACT.Sin, bias=quarter[:, 0:1])
        nc.scalar.activation(out=direction[:, 1, :], in_=angle[:, 1, :], func=ACT.Sin)
        turned_rows = psum_z.tile([P, POS_BLOCKS, P], BF16, tag="z")
        for b in range(POS_BLOCKS):
            nc.tensor.transpose(
                out=turned_rows[:, b, :], in_=position_rows[:, b * P : (b + 1) * P], identity=ident_bf[:]
            )
        by_axis = turned_rows[:, :, 0 : AXES * POS_ROWS].rearrange("q b (a m) -> q a m b", a=AXES)
        pos_squared = keep.tile([P, AXES, ROWS], F32)
        nc.scalar.activation(
            out=pos_squared[:].rearrange("q a (m b) -> q a m b", b=POS_BLOCKS), in_=by_axis, func=ACT.Square
        )
        nc.scalar.activation(out=warm_out[:], in_=warm[:], func=ACT.Exp)
        pos_scaled = keep.tile([P, AXES, ROWS], F32)
        nc.vector.tensor_scalar_mul(
            out=pos_scaled[:].rearrange("q a (m b) -> q a m b", b=POS_BLOCKS), in0=by_axis, scalar1=DIST_UNIT
        )
        inverse = keep.tile([P, N_DIST + N_SIGMA], F32)
        nc.vector.reciprocal(out=inverse[:], in_=one_plus[:])
        pick_terms = keep.tile([P, N_DIST], F32)
        nc.vector.tensor_mul(out=pick_terms[:], in0=one_plus[:, 0:N_DIST], in1=pick_dist[:])
        neg_norm2 = keep.tile([P, ROWS], F32)
        nc.vector.scalar_tensor_tensor(
            out=neg_norm2[:], in0=pos_squared[:, 0, :], scalar=-1.0, in1=pos_squared[:, 1, :],
            op0=ALU.mult, op1=ALU.subtract,
        )
        own = keep.tile([P, 1], F32)
        half_inv_var = keep.tile([P, N_SIGMA], F32)

        def make_own():
            nc.vector.tensor_reduce(out=own[:], in_=pick_terms[:], axis=AXIS_X, op=ALU.add)

        def make_half_inv_var():
            nc.vector.scalar_tensor_tensor(
                out=half_inv_var[:], in0=inverse[:, N_DIST:], scalar=0.5 / (HALF_UNIT * HALF_UNIT),
                in1=inverse[:, N_DIST:], op0=ALU.mult, op1=ALU.mult,
            )

        proj_terms = keep.tile([P, AXES, ROWS, N_PHI], F32)
        proj = keep.tile([P, ROWS, N_PHI], F32)

        def rows_of(first, count):
            return slice(first * ROWS_PER_NODE, (first + count) * ROWS_PER_NODE), count * ROWS_PER_NODE

        def project_terms(first, count):
            rows, n = rows_of(first, count)
            nc.vector.tensor_tensor(
                out=proj_terms[:, :, rows, :],
                in0=pos_scaled[:, :, rows].unsqueeze(3).to_broadcast([P, AXES, n, N_PHI]),
                in1=direction[:].unsqueeze(2).to_broadcast([P, AXES, n, N_PHI]),
                op=ALU.mult,
            )

        def project_sum(first, count):
            rows, n = rows_of(first, count)
            nc.vector.tensor_add(out=proj[:, rows, :], in0=proj_terms[:, 0, rows, :], in1=proj_terms[:, 1, rows, :])

        BOTH = (0, 1)
        z_cells, z_comps, gauss, gauss_sum, padded_sum, inv_sum = ({}, {}, {}, {}, {}, {})
        turned, grouped, products = ({}, {}, {})

        def new_z_cells(o):
            zc = work.tile([P, ROWS_PER_NODE, N_PHI, N_DIST], F32)
            z_cells[o] = zc

        def exponent_rows(o, first_row, n_rows, first_phi, n_phi):
            for r in range(first_row, first_row + n_rows):
                row = o * ROWS_PER_NODE + r
                nc.vector.scalar_tensor_tensor(
                    out=z_cells[o][:, r, first_phi : first_phi + n_phi, :],
                    in0=inverse[:, 0:N_DIST].unsqueeze(1).to_broadcast([P, n_phi, N_DIST]),
                    scalar=neg_norm2[:, row : row + 1],
                    in1=proj[:, row, first_phi : first_phi + n_phi].unsqueeze(2).to_broadcast([P, n_phi, N_DIST]),
                    op0=ALU.mult,
                    op1=ALU.add,
                )

        def turn_exponents(chunk):
            o, h = divmod(chunk, HALVES)
            z = psum_z.tile([P, CELLS], F32, tag="z")
            flat = z_cells[o][:].rearrange("q r p d -> q r (p d)")
            for r in range(ROWS_PER_NODE):
                nc.tensor.transpose(out=z[:, r * P : (r + 1) * P], in_=flat[:, r, h * P : (h + 1) * P], identity=ident[:])
            z_comps[chunk] = z

        exp_scale = keep.tile([P, N_SIGMA], F32)
        exp_bias = keep.tile([P, N_SIGMA], F32)

        def make_exp_scale():
            nc.vector.tensor_scalar_mul(out=exp_scale[:], in0=half_inv_var[:], scalar1=own[:, 0:1])

        def make_exp_bias():
            nc.vector.tensor_scalar(
                out=exp_bias[:], in0=exp_scale[:], scalar1=own[:, 0:1], scalar2=-HALF_UNIT * HALF_UNIT,
                op0=ALU.mult, op1=ALU.mult,
            )

        x_grouped = keep.tile([P, NODES * BATCH, CHANNELS, PACK], BF16, align_bytes=64)
        x_codes = keep.tile([P, NODES * COLS], U32, align_bytes=64)
        x_scales = keep.tile([P, NODES * COLS], U8, align_bytes=64)

        def regroup_x(first, count, on_scalar=False):
            rows = slice(first * BATCH, (first + count) * BATCH)
            by_column = x_raw[:].rearrange("q o b (t c) -> q (o b) c t", t=PACK)[:, rows]
            if on_scalar:
                nc.scalar.copy(out=x_grouped[:, rows], in_=by_column)
            else:
                nc.vector.tensor_copy(out=x_grouped[:, rows], in_=by_column)

        def quantise_x(first, count):
            rows = slice(first * BATCH, (first + count) * BATCH)
            cols = slice(first * COLS, (first + count) * COLS)
            nc.vector.quantize_mx(
                out=x_codes[:, cols].bitcast(FP8X4),
                scales=x_scales[:, cols],
                in_=x_grouped[:, rows].rearrange("q n c t -> q (n c t)"),
            )

        out_rows = out.rearrange("b o a p d s c -> b o (a p d s c)")

        def exps(chunk):
            g = work.tile([P, N_SIGMA, CELLS], F32)
            g_sum = work.tile([P, N_SIGMA], F32)
            for s in range(N_SIGMA):
                nc.scalar.activation(
                    out=g[:, s, :],
                    in_=z_comps[chunk][:],
                    func=ACT.Exp,
                    scale=exp_scale[:, s : s + 1],
                    bias=exp_bias[:, s : s + 1],
                    accum_out=g_sum[:, s : s + 1],
                )
            gauss[chunk] = g
            gauss_sum[chunk] = g_sum
            padded = work.tile([P, N_SIGMA], F32)
            padded_sum[chunk] = padded
            inv = work.tile([P, N_SIGMA], F32)
            inv_sum[chunk] = inv

        def add_eps(chunk, sigmas=BOTH):
            cols = slice(sigmas[0], sigmas[-1] + 1)
            nc.vector.tensor_scalar_add(out=padded_sum[chunk][:, cols], in0=gauss_sum[chunk][:, cols], scalar1=SUM_EPS)

        def invert_sums(chunk, sigmas=BOTH):
            cols = slice(sigmas[0], sigmas[-1] + 1)
            nc.vector.reciprocal(out=inv_sum[chunk][:, cols], in_=padded_sum[chunk][:, cols])

        def normalise_and_turn(chunk, sigmas=BOTH):
            weights = work.tile([P, len(sigmas), CELLS], BF16)
            for a, s in enumerate(sigmas):
                nc.vector.tensor_scalar_mul(
                    out=weights[:, a, :], in0=gauss[chunk][:, s, :], scalar1=inv_sum[chunk][:, s : s + 1]
                )
            words = weights[:].bitcast(F32)
            planes = psum_turned.tile([P, len(sigmas), PAIRS, P], F32)
            for a in range(len(sigmas)):
                for u in range(PAIRS):
                    nc.tensor.transpose(out=planes[:, a, u, :], in_=words[:, a, u * P : (u + 1) * P], identity=ident[:])
            turned[(chunk, sigmas)] = planes

        def regroup(chunk, sigmas=BOTH):
            grp = work.tile([P, len(sigmas), P, PAIRS], F32, align_bytes=64)
            nc.scalar.copy(out=grp[:], in_=turned[(chunk, sigmas)][:].rearrange("q s u j -> q s j u"))
            grouped[(chunk, sigmas)] = grp

        def quantise_and_multiply(chunk, sigmas=BOTH):
            o, h = divmod(chunk, HALVES)
            codes = work.tile([P, len(sigmas) * P], U32, align_bytes=64)
            scales = work.tile([P, len(sigmas) * P], U8, align_bytes=64)
            nc.vector.quantize_mx(
                out=codes[:].bitcast(FP8X4),
                scales=scales[:],
                in_=grouped[(chunk, sigmas)][:].rearrange("q s j u -> q (s j u)").bitcast(BF16),
            )
            product = psum_products.tile([P, CELLS], F32)
            products[(chunk, sigmas)] = product
            node_cols = slice(o * COLS, (o + 1) * COLS)
            for s in range(len(sigmas)):
                comp_cols = slice(s * P, (s + 1) * P)
                nc.tensor.matmul_mx(
                    out=product[:, s * COLS : (s + 1) * COLS],
                    lhsT=codes[:, comp_cols].bitcast(FP8X4),
                    lhsT_scale=scales[:, comp_cols],
                    rhs=x_codes[:, node_cols].bitcast(FP8X4),
                    rhs_scale=x_scales[:, node_cols],
                    start=True,
                    stop=True,
                )

        def store(chunk, sigmas=BOTH, on_scalar=None):
            o, h = divmod(chunk, HALVES)
            n = len(sigmas)
            result = outgoing.tile([P, BATCH, n, CHANNELS], F32)
            by_batch = products[(chunk, sigmas)][:, 0 : n * COLS].rearrange("j (s b c) -> j b s c", s=n, b=BATCH)
            if (chunk % 2 == 0) if on_scalar is None else on_scalar:
                nc.scalar.copy(out=result[:], in_=by_batch)
            else:
                nc.vector.tensor_copy(out=result[:], in_=by_batch)
            span = P * N_SIGMA * CHANNELS
            half_rows = out_rows[:, o, h * span : (h + 1) * span]
            if n == N_SIGMA:
                nc.sync.dma_start(
                    out=half_rows.rearrange("b (j f) -> j b f", j=P), in_=result[:].rearrange("j b s c -> j b (s c)")
                )
            else:
                nc.sync.dma_start(
                    out=half_rows.rearrange("b (j s c) -> j b s c", j=P, s=N_SIGMA)[:, :, sigmas[0], :],
                    in_=result[:, :, 0, :],
                )

        regroup_x(0, 1, on_scalar=True)
        project_terms(0, 1)
        make_own()
        make_half_inv_var()
        project_sum(0, 1)
        make_exp_scale()
        new_z_cells(0)
        project_terms(1, 1)
        for r in range(ROWS_PER_NODE):
            exponent_rows(0, r, 1, 0, PHI_PER_HALF)
        turn_exponents(0)
        make_exp_bias()
        exponent_rows(0, 0, 2, PHI_PER_HALF, PHI_PER_HALF)
        project_sum(1, 1)
        exponent_rows(0, 2, 2, PHI_PER_HALF, PHI_PER_HALF)
        new_z_cells(1)
        exponent_rows(1, 0, 2, 0, N_PHI)

        def z_part(i):
            node = (i + 3) // 2
            if i % 2 == 1:
                new_z_cells(node)
                exponent_rows(node, 0, 2, 0, N_PHI)
            else:
                exponent_rows(node, 2, 2, 0, N_PHI)

        for i in range(CHUNKS - 1):
            has_z = (i + 3) // 2 < NODES
            turn_exponents(i + 1)
            exps(i)
            if i >= 1:
                add_eps(i - 1)
            if i == 1:
                project_terms(2, NODES - 2)
            if i == 2:
                z_part(i)
            if i >= 3:
                quantise_and_multiply(i - 3)
            if i >= 1:
                invert_sums(i - 1)
            if i == 1:
                project_sum(2, NODES - 2)
            if i == 2:
                quantise_x(0, 1)
            if i == 3:
                regroup_x(1, 1)
            z_early = i >= 4 and i % 2 == 0 and has_z
            if i >= 4 and i % 2 == 1:
                store(i - 4)
            if z_early:
                z_part(i)
            if i >= 1:
                normalise_and_turn(i - 1)
            if has_z and i != 2 and not z_early:
                z_part(i)
            if i % 2 == 1 and i >= 5:
                regroup_x(i // 2, 1)
            if i % 2 == 0 and i >= 4:
                quantise_x(i // 2 - 1, 1)
            if i >= 2:
                regroup(i - 2)
            if i >= 4 and i % 2 == 0:
                store(i - 4)

        last = CHUNKS - 1
        exps(last)
        add_eps(last - 1)
        regroup_x(NODES - 1, 1)
        invert_sums(last - 1)
        store(last - 4, on_scalar=False)
        normalise_and_turn(last - 1)
        add_eps(last, (0,))
        quantise_and_multiply(last - 3)
        invert_sums(last, (0,))
        quantise_x(NODES - 1, 1)
        regroup(last - 2)
        add_eps(last, (1,))
        normalise_and_turn(last, (0,))
        invert_sums(last, (1,))
        store(last - 3, on_scalar=True)
        normalise_and_turn(last, (1,))
        regroup(last - 1)
        quantise_and_multiply(last - 2)
        quantise_and_multiply(last - 1)
        regroup(last, (0,))
        store(last - 2)
        quantise_and_multiply(last, (0,))
        regroup(last, (1,))
        store(last - 1)
        quantise_and_multiply(last, (1,))
        store(last, (0,), on_scalar=True)
        store(last, (1,), on_scalar=False)
